import numpy as np
import ml_dtypes


def mxq(x, axis, fmt="e4m3"):
    dtype, down = {"e4m3": (ml_dtypes.float8_e4m3fn, 7), "e5m2": (ml_dtypes.float8_e5m2, 14)}[fmt]
    v = np.moveaxis(np.asarray(x, np.float32).astype(ml_dtypes.bfloat16).astype(np.float64), axis, -1)
    blocks = v.reshape(v.shape[:-1] + (-1, 32))
    amax = np.abs(blocks).max(-1, keepdims=True)
    byte = np.maximum(np.where(amax > 0, np.frexp(amax)[1] - 1 + 127, 0) - down, 1)
    scale = np.exp2(byte - 127.0)
    codes = (blocks / scale).astype(np.float32).astype(dtype).astype(np.float64)
    return np.moveaxis((codes * scale).reshape(v.shape), -1, axis)


WIDE = False


def mx_kscale(k):
    if not WIDE:
        return np.ones(k)
    levels = np.array([10, -10, 5, -5, 0])
    if k % 512:
        return np.exp2(np.random.permutation(np.resize(levels, k // 32))).repeat(32)
    a = np.empty((k // 512, 16))
    for p in range(k // 512):
        a[p, :8] = np.random.permutation(np.resize(levels, 8))
        for g in range(8):
            far = levels[np.abs(levels - a[p, g]) >= 10]
            a[p, g + 8] = far[np.random.randint(len(far))]
    return np.exp2(a.ravel()).repeat(32)


BF16 = ml_dtypes.bfloat16


def bf(x):
    return np.asarray(x, np.float32).astype(BF16)


def f64(x):
    return np.asarray(x).astype(np.float64)


NB, S, D, O, E, R = 4, 128, 2048, 2048, 32, 16
ER = E * R
SCALING = 2.0


def softmax(v):
    e = np.exp(v - v.max(-1, keepdims=True))
    return e / e.sum(-1, keepdims=True)


def setup_inputs():
    s, t = mx_kscale(D), mx_kscale(ER)
    return {
        "x": bf(np.random.standard_normal((NB, S, D)) * s),
        "gate_logits": bf(np.random.standard_normal((NB, S, E)) * 1.5),
        "W_base": bf(np.random.standard_normal((O, D)) / np.sqrt(D) / s),
        "b_base": bf(np.random.standard_normal(O) * 0.3),
        "A": bf(np.random.standard_normal((E, R, D)) / np.sqrt(D) / s * t.reshape(E, R, 1)),
        "B": bf(np.random.standard_normal((E, O, R)) / np.sqrt(R) / t.reshape(E, 1, R)),
    }


def reference(x, gate_logits, W_base, b_base, A, B):
    xq = mxq(f64(x), 2, "e4m3")
    result = (xq @ mxq(f64(W_base), 1, "e4m3").T) + f64(b_base)
    route = softmax(f64(gate_logits))
    h = (xq @ mxq(f64(A).reshape(ER, D), 1, "e4m3").T).reshape(NB, S, E, R)
    hw = (h * route[..., None]).reshape(NB, S, ER)
    b_flat = f64(B).transpose(0, 2, 1).reshape(ER, O)
    return result + SCALING * (mxq(hw, 2, "e4m3") @ mxq(b_flat, 0, "e4m3"))

@@ -1,0 +1,443 @@
+from contextlib import ExitStack
+
+import concourse.mybir as mybir
+from concourse.masks import make_identity
+
+F32 = mybir.dt.float32
+BF16 = mybir.dt.bfloat16
+U32 = mybir.dt.uint32
+U8 = mybir.dt.uint8
+I32 = mybir.dt.int32
+FP8X4 = mybir.dt.float8_e4m3fn_x4
+ALU = mybir.AluOpType
+ACT = mybir.ActivationFunctionType
+AX = mybir.AxisListType
+
+P = 128
+TT = 4
+D = 2048
+O = 2048
+E = 32
+R = 16
+NG = 4
+NC = 4
+FLOPS = 2 * 512 * D * O + 2 * 512 * D * 512 + 2 * 512 * 512 * O
+DEFERRED = (0,)
+
+
+def tile_linearmoloralayer_pa_kernel(tc, x, gate_logits, W_base, b_base, A, B, out):
+    nc = tc.nc
+    xf = x.flatten_outer_dims()
+    gf = gate_logits.flatten_outer_dims()
+    af = A.flatten_outer_dims().rearrange("(p t) d -> t p d", t=4)
+    of = out.flatten_outer_dims()
+
+    with ExitStack() as ctx:
+        const = ctx.enter_context(tc.tile_pool(name="const", bufs=1))
+        rawp = ctx.enter_context(tc.tile_pool(name="rawp", bufs=8))
+        grpp = ctx.enter_context(tc.tile_pool(name="grpp", bufs=3))
+        bsp = ctx.enter_context(tc.tile_pool(name="bsp", bufs=6))
+        wcp = ctx.enter_context(tc.tile_pool(name="wcp", bufs=3))
+        outp = ctx.enter_context(tc.tile_pool(name="outp", bufs=4))
+        accp = ctx.enter_context(tc.psum_pool(name="accp", bufs=1))
+        stp = ctx.enter_context(tc.psum_pool(name="stp", bufs=4))
+        ctx.enter_context(tc.manual_schedule())
+
+        ident = const.tile([P, P], F32)
+        make_identity(nc, ident[:])
+        brow = bsp.tile([P, O], BF16, tag="bs")
+        nc.vector.memset(brow[:].bitcast(I32), 0)
+        nc.sync.dma_start(out=brow[0:1, :], in_=b_base.rearrange("(o n) -> o n", o=1))
+        zeros = const.tile([P, 512], BF16)
+        nc.vector.memset(zeros[:].bitcast(I32), 0)
+        ones = const.tile([P, P], BF16)
+        nc.vector.memset(ones[:], 1.0)
+        warm = const.tile([P, 1], F32)
+        nc.vector.memset(warm[:], 0.0)
+        nc.scalar.activation(out=warm[:], in_=warm[:], func=ACT.Exp)
+
+        raws = {}
+        gl = const.tile([P, TT, E], BF16)
+        for t in range(TT):
+            r = rawp.tile([P, 4096], BF16, tag="raw")
+            nc.sync.dma_start(out=r[:, D:2 * D], in_=af[t, :, :])
+            nc.sync.dma_start(out=r[:, 0:D], in_=xf[t * P:(t + 1) * P, :])
+            raws[("xa", t)] = r
+            if t == 0:
+                nc.sync.dma_start(out=gl[:], in_=gf.rearrange("(t p) e -> p t e", p=P))
+        bview = B.rearrange("e (p s) r -> p e (s r)", s=16)
+
+        def load_w(c, d):
+            r = rawp.tile([P, 4096], BF16, tag="raw")
+            nc.sync.dma_start(
+                out=r[:].rearrange("p (j k) -> p j k", j=4),
+                in_=W_base[c * 512:(c + 1) * 512, d * 1024:(d + 1) * 1024].rearrange("(j p) k -> p j k", p=P),
+            )
+            raws[("w", c, d)] = r
+
+        bias_bc = const.tile([P, O], F32)
+
+        def load_b(h):
+            r = rawp.tile([P, 4096], BF16, tag="raw")
+            nc.sync.dma_start(out=r[:].rearrange("p (e k) -> p e k", e=16), in_=bview[:, 16 * h:16 * h + 16, :])
+            raws[("b", h)] = r
+
+        load_w(0, 0)
+        load_w(0, 1)
+        load_w(1, 0)
+        load_b(0)
+
+        xc = const.tile([P, TT, 512], U32, align_bytes=64)
+        xs = const.tile([P, TT, 512], U8, align_bytes=64)
+        ac = const.tile([P, 4, 512], U32, align_bytes=64)
+        asc = const.tile([P, 4, 512], U8, align_bytes=64)
+        bc = const.tile([P, O], U32, align_bytes=64)
+        bsc = const.tile([P, O], U8, align_bytes=64)
+        hc = const.tile([P, 512], U32, align_bytes=64)
+        hsc = const.tile([P, 512], U8, align_bytes=64)
+        hwg = const.tile([P, 2048], BF16, align_bytes=64)
+        bg = const.tile([P, 4 * O], BF16, align_bytes=64)
+        rt = const.tile([P, TT, P], F32)
+        bs = const.tile([P, 16, 2, P], F32)
+        keep = const.tile([P, len(DEFERRED) * TT, 512], F32)
+
+        rexp = bsp.tile([P, TT, E, 4], F32, tag="bs")
+
+        ex = const.tile([P, TT, E], F32)
+
+        def softmax_head():
+            mx = const.tile([P, TT], F32)
+            nc.vector.tensor_reduce(out=mx[:], in_=gl[:], axis=AX.X, op=ALU.max)
+            dl = const.tile([P, TT, E], F32)
+            nc.vector.tensor_tensor(out=dl[:], in0=gl[:], in1=mx[:].unsqueeze(2).to_broadcast([P, TT, E]), op=ALU.subtract)
+            nc.scalar.activation(out=ex[:], in_=dl[:], func=ACT.Exp)
+
+        def softmax_tail():
+            sm = const.tile([P, TT], F32)
+            nc.vector.tensor_reduce(out=sm[:], in_=ex[:], axis=AX.X, op=ALU.add)
+            rc = const.tile([P, TT], F32)
+            nc.vector.reciprocal(out=rc[:], in_=sm[:])
+            rc2 = const.tile([P, TT], F32)
+            nc.vector.tensor_scalar_mul(out=rc2[:], in0=rc[:], scalar1=2.0)
+            nc.vector.tensor_tensor(
+                out=rexp[:],
+                in0=ex[:].unsqueeze(3).to_broadcast([P, TT, E, 4]),
+                in1=rc2[:].unsqueeze(2).unsqueeze(3).to_broadcast([P, TT, E, 4]),
+                op=ALU.mult,
+            )
+
+        grps = {}
+        wcs = {}
+        accs = {}
+
+        def dummy(st):
+            nc.tensor.matmul(out=st[:], lhsT=ones[:], rhs=zeros[:], start=True, stop=True)
+
+        def warm_up(n):
+            st = stp.tile([P, 512], F32, tag="st")
+            for i in range(n):
+                dummy(st)
+
+        def bias_job(cs):
+            for c in cs:
+                st = stp.tile([P, 512], F32, tag="st")
+                nc.tensor.matmul(out=st[:], lhsT=ones[:], rhs=brow[:, c * 512:(c + 1) * 512], start=True, stop=True)
+                if c % 2 == 0:
+                    nc.vector.tensor_copy(out=bias_bc[:, c * 512:(c + 1) * 512], in_=st[:])
+                else:
+                    nc.scalar.copy(out=bias_bc[:, c * 512:(c + 1) * 512], in_=st[:])
+
+        def flip_bank(views, words, eng, ndummy=0):
+            st = stp.tile([P, 512], F32, tag="st")
+            for i in range(ndummy):
+                dummy(st)
+            for s in range(4):
+                nc.tensor.transpose(st[:, s * P:(s + 1) * P], views[s], ident[:])
+            src = st[:].rearrange("p (j u n) -> p j n u", j=2, u=2)
+            dst = words.rearrange("p (j n u) -> p j n u", j=2, u=2)
+            if eng == "v":
+                nc.vector.tensor_copy(out=dst, in_=src)
+            else:
+                nc.scalar.copy(out=dst, in_=src)
+
+        def t_xa(kind, t, nd=(0, 0)):
+            grp = grpp.tile([P, 2048], BF16, tag="grp", align_bytes=64)
+            grps[(kind, t)] = grp
+            w = raws[("xa", t)][:].bitcast(F32)
+            base = 0 if kind == "x" else 1024
+            words = grp[:].bitcast(F32)
+            for b in range(2):
+                flip_bank([w[:, base + 512 * b + 256 * (s // 2) + s % 2:base + 512 * b + 256 * (s // 2 + 1):2] for s in range(4)], words[:, 512 * b:512 * (b + 1)], "s", nd[b])
+
+        def q_xa(kind, t):
+            codes, scales = (xc, xs) if kind == "x" else (ac, asc)
+            nc.vector.quantize_mx(out=codes[:, t, :].bitcast(FP8X4), scales=scales[:, t, :], in_=grps[(kind, t)][:])
+
+        def t_w(c, d, engs="ssss"):
+            grp = grpp.tile([P, 4096], BF16, tag="grp", align_bytes=64)
+            grps[("w", c, d)] = grp
+            w = raws[("w", c, d)][:].bitcast(F32)
+            words = grp[:].bitcast(F32)
+            for k in range(2):
+                for b in range(2):
+                    views = [w[:, (2 * b + s // 2) * 512 + k * 256 + s % 2:(2 * b + s // 2) * 512 + (k + 1) * 256:2] for s in range(4)]
+                    flip_bank(views, words[:, 1024 * k + 512 * b:1024 * k + 512 * (b + 1)], engs[2 * k + b])
+
+        def q_w(c, d):
+            wc = wcp.tile([P, 1024], U32, tag="wc", align_bytes=64)
+            ws = wcp.tile([P, 1024], U8, tag="ws", align_bytes=64)
+            wcs[(c, d)] = (wc, ws)
+            for k in range(2):
+                nc.vector.quantize_mx(
+                    out=wc[:, k * 512:(k + 1) * 512].bitcast(FP8X4),
+                    scales=ws[:, k * 512:(k + 1) * 512],
+                    in_=grps[("w", c, d)][:, k * 2048:(k + 1) * 2048],
+                )
+
+        def new_acc(key):
+            tiles = []
+            for tt in range(TT):
+                a = accp.tile([P, 512], F32, tag="acc%d" % tt, name="acc%d" % tt)
+                tiles.append(a)
+            accs[key] = tiles
+            return tiles
+
+        def route_job():
+            rw = rexp[:].rearrange("p t e i -> p t (e i)")
+            st = stp.tile([P, 512], F32, tag="st")
+            for t in range(TT):
+                nc.tensor.transpose(st[:, t * P:(t + 1) * P], rw[:, t, :], ident[:])
+            nc.scalar.copy(out=rt[:].rearrange("p t n -> p (t n)"), in_=st[:])
+
+        def h_group(t, tt):
+            hps = accs["h"]
+            for g in range(NG):
+                nc.tensor.matmul_mx(
+                    out=hps[tt][:, t * P:(t + 1) * P],
+                    lhsT=ac[:, t, g * P:(g + 1) * P].bitcast(FP8X4),
+                    lhsT_scale=asc[:, t, g * P:(g + 1) * P],
+                    rhs=xc[:, tt, g * P:(g + 1) * P].bitcast(FP8X4),
+                    rhs_scale=xs[:, tt, g * P:(g + 1) * P],
+                    start=(g == 0),
+                    stop=(g == NG - 1),
+                )
+
+        def hw_mult(tt):
+            nc.vector.tensor_tensor(
+                out=hwg[:, tt * 512:(tt + 1) * 512].rearrange("p (n t) -> p n t", t=4),
+                in0=accs["h"][tt][:].rearrange("p (t n) -> p n t", t=4),
+                in1=rt[:, tt, :].unsqueeze(2).to_broadcast([P, P, 4]),
+                op=ALU.mult,
+            )
+
+        def hw_quant():
+            nc.vector.quantize_mx(out=hc[:].bitcast(FP8X4), scales=hsc[:], in_=hwg[:])
+
+        def shuffle_b(h):
+            src = raws[("b", h)][:].bitcast(F32).rearrange("p (e s v u) -> p u s e v", e=16, s=16, v=4)
+            dst = bs[:].rearrange("p s u (e v) -> p u s e v", v=4)
+            for u in range(2):
+                nc.vector.tensor_copy(out=dst[:, u, :, 16 * h:16 * h + 16, :], in_=src[:, u])
+
+        def t_b(half, engs):
+            bgw = bg[:].bitcast(F32).rearrange("p (n s u) -> p n s u", s=16, u=2)
+            for q in (2 * half, 2 * half + 1):
+                for b in range(2):
+                    st = stp.tile([P, 512], F32, tag="st")
+                    s0 = 4 * q + 2 * b
+                    for i in range(4):
+                        nc.tensor.transpose(st[:, i * P:(i + 1) * P], bs[:, s0 + i // 2, i % 2, :], ident[:])
+                    src = st[:].rearrange("p (s u n) -> p n s u", s=2, u=2)
+                    if engs[q % 2] == "v":
+                        nc.vector.tensor_copy(out=bgw[:, :, s0:s0 + 2, :], in_=src)
+                    else:
+                        nc.scalar.copy(out=bgw[:, :, s0:s0 + 2, :], in_=src)
+
+        def q_b(hs):
+            for h in hs:
+                nc.vector.quantize_mx(
+                    out=bc[:, h * 1024:(h + 1) * 1024].bitcast(FP8X4),
+                    scales=bsc[:, h * 1024:(h + 1) * 1024],
+                    in_=bg[:, h * 4096:(h + 1) * 4096],
+                )
+
+        def lora_pass(dst, c, tt, start, stop):
+            nc.tensor.matmul_mx(
+                out=dst[:],
+                lhsT=hc[:, tt * P:(tt + 1) * P].bitcast(FP8X4),
+                lhsT_scale=hsc[:, tt * P:(tt + 1) * P],
+                rhs=bc[:, c * 512:(c + 1) * 512].bitcast(FP8X4),
+                rhs_scale=bsc[:, c * 512:(c + 1) * 512],
+                start=start,
+                stop=stop,
+            )
+
+        def base_pass(c, g, tt, start, stop):
+            wc, ws = wcs[(c, g // 2)]
+            k = g % 2
+            nc.tensor.matmul_mx(
+                out=accs[c][tt][:],
+                lhsT=xc[:, tt, g * P:(g + 1) * P].bitcast(FP8X4),
+                lhsT_scale=xs[:, tt, g * P:(g + 1) * P],
+                rhs=wc[:, k * 512:(k + 1) * 512].bitcast(FP8X4),
+                rhs_scale=ws[:, k * 512:(k + 1) * 512],
+                start=start,
+                stop=stop,
+            )
+
+        def store(c, tt, src):
+            nc.sync.dma_start(out=of[tt * P:(tt + 1) * P, c * 512:(c + 1) * 512], in_=src)
+
+        def p4(c, g):
+            if g == 0:
+                new_acc(c)
+            for tt in range(TT):
+                base_pass(c, g, tt, g == 0, False)
+
+        def evac(c, tt):
+            if c in DEFERRED:
+                dst = keep[:, DEFERRED.index(c) * TT + tt, :]
+            else:
+                osb = outp.tile([P, 512], F32, tag="osb")
+                dst = osb[:]
+            nc.vector.tensor_tensor(out=dst, in0=accs[c][tt][:], in1=bias_bc[:, c * 512:(c + 1) * 512], op=ALU.add)
+            if c not in DEFERRED:
+                store(c, tt, dst)
+
+        def p_close(c, gs, tts):
+            late = c in DEFERRED
+            for tt in tts:
+                for g in gs:
+                    base_pass(c, g, tt, False, late and g == NG - 1)
+                if not late:
+                    lora_pass(accs[c][tt], c, tt, False, True)
+                evac(c, tt)
+
+        def p4_some(c, g, tts):
+            if g == 0:
+                new_acc(c)
+            for tt in tts:
+                base_pass(c, g, tt, g == 0, False)
+
+        def last_tile_in_halves(c, tt):
+            for half in range(2):
+                if half == 0:
+                    bank = accs[c][tt]
+                else:
+                    bank = stp.tile([P, 512], F32, tag="st", name="lasthalf")
+                cols = slice(c * 512 + half * 256, c * 512 + (half + 1) * 256)
+                for g in range(NG):
+                    wc, ws = wcs[(c, g // 2)]
+                    wcols = slice((g % 2) * 512 + half * 256, (g % 2) * 512 + (half + 1) * 256)
+                    nc.tensor.matmul_mx(
+                        out=bank[:, 0:256],
+                        lhsT=xc[:, tt, g * P:(g + 1) * P].bitcast(FP8X4),
+                        lhsT_scale=xs[:, tt, g * P:(g + 1) * P],
+                        rhs=wc[:, wcols].bitcast(FP8X4),
+                        rhs_scale=ws[:, wcols],
+                        start=(g == 0),
+                        stop=False,
+                    )
+                nc.tensor.matmul_mx(
+                    out=bank[:, 0:256],
+                    lhsT=hc[:, tt * P:(tt + 1) * P].bitcast(FP8X4),
+                    lhsT_scale=hsc[:, tt * P:(tt + 1) * P],
+                    rhs=bc[:, cols].bitcast(FP8X4),
+                    rhs_scale=bsc[:, cols],
+                    start=False,
+                    stop=True,
+                )
+                osb = outp.tile([P, 256], F32, tag="osb")
+                nc.vector.tensor_tensor(out=osb[:], in0=bank[:, 0:256], in1=bias_bc[:, cols], op=ALU.add)
+                nc.sync.dma_start(out=of[tt * P:(tt + 1) * P, cols], in_=osb[:])
+
+        def late_lora(c, where):
+            banks = []
+            for tt in range(TT):
+                if where == "acc":
+                    a = accp.tile([P, 512], F32, tag="acc%d" % tt, name="late%d" % tt)
+                else:
+                    a = stp.tile([P, 512], F32, tag="st", name="late")
+                banks.append(a)
+                lora_pass(a, c, tt, True, True)
+            for tt in range(TT):
+                osb = outp.tile([P, 512], F32, tag="osb")
+                nc.vector.tensor_tensor(out=osb[:], in0=banks[tt][:], in1=keep[:, DEFERRED.index(c) * TT + tt, :], op=ALU.add)
+                store(c, tt, osb[:])
+
+        arr = []
+        for t in range(TT):
+            arr.append(("a", t))
+            arr.append(("x", t))
+        done = []
+        new_acc("h")
+        warm_up(5)
+        bias_job((0, 1, 2, 3))
+        for k in range(len(arr) + 2):
+            if k < len(arr):
+                t_xa(arr[k][0], arr[k][1], (1, 0) if k < 5 else (0, 0))
+            if k == 2:
+                softmax_head()
+            if k == 4:
+                softmax_tail()
+            if k == 5:
+                route_job()
+            if k == 8:
+                load_w(1, 1)
+                load_b(1)
+                load_w(2, 0)
+                load_w(2, 1)
+                t_w(0, 0)
+            if 1 <= k <= len(arr):
+                q_xa(arr[k - 1][0], arr[k - 1][1])
+            if k == 9:
+                q_w(0, 0)
+                t_w(0, 1)
+            if 2 <= k:
+                done.append(arr[k - 2])
+                for t2 in range(TT):
+                    for t1 in range(4):
+                        if ("a", t1) in done and ("x", t2) in done and (t1, t2) not in done:
+                            done.append((t1, t2))
+                            h_group(t1, t2)
+                            if t1 == 3:
+                                hw_mult(t2)
+
+        hw_quant()
+        p4(0, 0)
+        p4(0, 1)
+        q_w(0, 1)
+        shuffle_b(0)
+        t_w(1, 0)
+        load_w(3, 0)
+        p_close(0, (2, 3), (0, 1))
+        q_w(1, 0)
+        p_close(0, (2, 3), (2, 3))
+        t_w(1, 1)
+        load_w(3, 1)
+        shuffle_b(1)
+        p4(1, 0)
+        q_w(1, 1)
+        t_b(0, "ss")
+        p4(1, 1)
+        t_b(1, "sv")
+        p4(1, 2)
+        t_w(2, 0)
+        q_b((0,))
+        p4(1, 3)
+        q_w(2, 0)
+        p_close(1, (), (0, 1, 2, 3))
+        t_w(2, 1)
+        late_lora(0, "acc")
+        q_w(2, 1)
+        t_w(3, 0)
+        q_b((1,))
+        p4(2, 0)
+        p4(2, 1)
+        q_w(3, 0)
+        t_w(3, 1)
+        p_close(2, (2, 3), (0, 1, 2, 3))
+        q_w(3, 1)
+        p4(3, 0)
+        p4(3, 1)
+        p_close(3, (2, 3), (0, 1, 2, 3))

@@ -22,7 +22,7 @@ R = 16
 NG = 4
 NC = 4
 FLOPS = 2 * 512 * D * O + 2 * 512 * D * 512 + 2 * 512 * 512 * O
-DEFERRED = (0,)
+WARM = 3
 
 
 def tile_linearmoloralayer_pa_kernel(tc, x, gate_logits, W_base, b_base, A, B, out):
@@ -31,41 +31,34 @@ def tile_linearmoloralayer_pa_kernel(tc, x, gate_logits, W_base, b_base, A, B, o
     gf = gate_logits.flatten_outer_dims()
     af = A.flatten_outer_dims().rearrange("(p t) d -> t p d", t=4)
     of = out.flatten_outer_dims()
+    bview = B.rearrange("e (p s) r -> p e (s r)", s=16)
 
     with ExitStack() as ctx:
         const = ctx.enter_context(tc.tile_pool(name="const", bufs=1))
-        rawp = ctx.enter_context(tc.tile_pool(name="rawp", bufs=8))
+        rawp = ctx.enter_context(tc.tile_pool(name="rawp", bufs=9))
+        dip = ctx.enter_context(tc.tile_pool(name="dip", bufs=3))
         grpp = ctx.enter_context(tc.tile_pool(name="grpp", bufs=3))
-        bsp = ctx.enter_context(tc.tile_pool(name="bsp", bufs=6))
         wcp = ctx.enter_context(tc.tile_pool(name="wcp", bufs=3))
         outp = ctx.enter_context(tc.tile_pool(name="outp", bufs=4))
         accp = ctx.enter_context(tc.psum_pool(name="accp", bufs=1))
         stp = ctx.enter_context(tc.psum_pool(name="stp", bufs=4))
         ctx.enter_context(tc.manual_schedule())
 
-        ident = const.tile([P, P], F32)
-        make_identity(nc, ident[:])
-        brow = bsp.tile([P, O], BF16, tag="bs")
-        nc.vector.memset(brow[:].bitcast(I32), 0)
-        nc.sync.dma_start(out=brow[0:1, :], in_=b_base.rearrange("(o n) -> o n", o=1))
-        zeros = const.tile([P, 512], BF16)
-        nc.vector.memset(zeros[:].bitcast(I32), 0)
-        ones = const.tile([P, P], BF16)
-        nc.vector.memset(ones[:], 1.0)
-        warm = const.tile([P, 1], F32)
-        nc.vector.memset(warm[:], 0.0)
-        nc.scalar.activation(out=warm[:], in_=warm[:], func=ACT.Exp)
-
         raws = {}
-        gl = const.tile([P, TT, E], BF16)
-        for t in range(TT):
+        dis = {}
+        grps = {}
+        wcs = {}
+        accs = {}
+
+        def load_a(t):
+            nc.sync.dma_start(out=raws[("xa", t)][:, D:2 * D], in_=af[t, :, :])
+
+        def load_x(t):
+            nc.sync.dma_start(out=raws[("xa", t)][:, 0:D], in_=xf[t * P:(t + 1) * P, :])
+
+        def raw_xa(t):
             r = rawp.tile([P, 4096], BF16, tag="raw")
-            nc.sync.dma_start(out=r[:, D:2 * D], in_=af[t, :, :])
-            nc.sync.dma_start(out=r[:, 0:D], in_=xf[t * P:(t + 1) * P, :])
             raws[("xa", t)] = r
-            if t == 0:
-                nc.sync.dma_start(out=gl[:], in_=gf.rearrange("(t p) e -> p t e", p=P))
-        bview = B.rearrange("e (p s) r -> p e (s r)", s=16)
 
         def load_w(c, d):
             r = rawp.tile([P, 4096], BF16, tag="raw")
@@ -75,17 +68,35 @@ def tile_linearmoloralayer_pa_kernel(tc, x, gate_logits, W_base, b_base, A, B, o
             )
             raws[("w", c, d)] = r
 
-        bias_bc = const.tile([P, O], F32)
-
         def load_b(h):
             r = rawp.tile([P, 4096], BF16, tag="raw")
             nc.sync.dma_start(out=r[:].rearrange("p (e k) -> p e k", e=16), in_=bview[:, 16 * h:16 * h + 16, :])
             raws[("b", h)] = r
 
+        ident = const.tile([P, P], F32)
+        make_identity(nc, ident[:])
+        zeros = const.tile([P, 512], BF16)
+        nc.vector.memset(zeros[:].bitcast(I32), 0)
+        ones = const.tile([P, P], BF16)
+        nc.vector.memset(ones[:], 1.0)
+        warm = const.tile([P, 1], F32)
+        nc.vector.memset(warm[:], 0.0)
+        nc.scalar.activation(out=warm[:], in_=warm[:], func=ACT.Exp)
+
+        gl = const.tile([P, TT, E], BF16)
+        for t in range(TT):
+            raw_xa(t)
+            load_x(t)
+            if t == 0:
+                nc.sync.dma_start(out=gl[:], in_=gf.rearrange("(t p) e -> p t e", p=P))
+        for t in range(TT):
+            load_a(t)
         load_w(0, 0)
         load_w(0, 1)
+        bias_bc = const.tile([P, O], BF16)
+        nc.sync.dma_start(out=bias_bc[:], in_=b_base.partition_broadcast(P))
         load_w(1, 0)
-        load_b(0)
+        load_w(1, 1)
 
         xc = const.tile([P, TT, 512], U32, align_bytes=64)
         xs = const.tile([P, TT, 512], U8, align_bytes=64)
@@ -97,13 +108,17 @@ def tile_linearmoloralayer_pa_kernel(tc, x, gate_logits, W_base, b_base, A, B, o
         hsc = const.tile([P, 512], U8, align_bytes=64)
         hwg = const.tile([P, 2048], BF16, align_bytes=64)
         bg = const.tile([P, 4 * O], BF16, align_bytes=64)
-        rt = const.tile([P, TT, P], F32)
         bs = const.tile([P, 16, 2, P], F32)
-        keep = const.tile([P, len(DEFERRED) * TT, 512], F32)
-
-        rexp = bsp.tile([P, TT, E, 4], F32, tag="bs")
-
+        rt = const.tile([P, TT, P], F32)
+        rexp = const.tile([P, TT, E, 4], F32)
         ex = const.tile([P, TT, E], F32)
+        keep = const.tile([P, TT, 512], F32)
+
+        def copy(eng, out_ap, in_ap):
+            if eng == "v":
+                nc.vector.tensor_copy(out=out_ap, in_=in_ap)
+            else:
+                nc.scalar.copy(out=out_ap, in_=in_ap)
 
         def softmax_head():
             mx = const.tile([P, TT], F32)
@@ -126,10 +141,6 @@ def tile_linearmoloralayer_pa_kernel(tc, x, gate_logits, W_base, b_base, A, B, o
                 op=ALU.mult,
             )
 
-        grps = {}
-        wcs = {}
-        accs = {}
-
         def dummy(st):
             nc.tensor.matmul(out=st[:], lhsT=ones[:], rhs=zeros[:], start=True, stop=True)
 
@@ -138,56 +149,69 @@ def tile_linearmoloralayer_pa_kernel(tc, x, gate_logits, W_base, b_base, A, B, o
             for i in range(n):
                 dummy(st)
 
-        def bias_job(cs):
-            for c in cs:
-                st = stp.tile([P, 512], F32, tag="st")
-                nc.tensor.matmul(out=st[:], lhsT=ones[:], rhs=brow[:, c * 512:(c + 1) * 512], start=True, stop=True)
-                if c % 2 == 0:
-                    nc.vector.tensor_copy(out=bias_bc[:, c * 512:(c + 1) * 512], in_=st[:])
-                else:
-                    nc.scalar.copy(out=bias_bc[:, c * 512:(c + 1) * 512], in_=st[:])
-
         def flip_bank(views, words, eng, ndummy=0):
             st = stp.tile([P, 512], F32, tag="st")
             for i in range(ndummy):
                 dummy(st)
             for s in range(4):
                 nc.tensor.transpose(st[:, s * P:(s + 1) * P], views[s], ident[:])
-            src = st[:].rearrange("p (j u n) -> p j n u", j=2, u=2)
-            dst = words.rearrange("p (j n u) -> p j n u", j=2, u=2)
-            if eng == "v":
-                nc.vector.tensor_copy(out=dst, in_=src)
-            else:
-                nc.scalar.copy(out=dst, in_=src)
+            copy(eng, words.rearrange("p (j n u) -> p j n u", j=2, u=2), st[:].rearrange("p (j u n) -> p j n u", j=2, u=2))
 
-        def t_xa(kind, t, nd=(0, 0)):
+        def xa_words(kind, t):
+            base = 0 if kind == "x" else 1024
+            return raws[("xa", t)][:].bitcast(F32)[:, base:base + 1024]
+
+        def d_xa(kind, t, eng="v"):
+            di = dip.tile([P, 2048], F32, tag="di")
+            dis[(kind, t)] = di
+            copy(eng, di[:, 0:1024].rearrange("p (g u n) -> p g u n", g=4, u=2), xa_words(kind, t).rearrange("p (g n u) -> p g u n", g=4, u=2))
+
+        def t_xa(kind, t, nd=(0, 0), engs="ss"):
             grp = grpp.tile([P, 2048], BF16, tag="grp", align_bytes=64)
             grps[(kind, t)] = grp
-            w = raws[("xa", t)][:].bitcast(F32)
-            base = 0 if kind == "x" else 1024
             words = grp[:].bitcast(F32)
             for b in range(2):
-                flip_bank([w[:, base + 512 * b + 256 * (s // 2) + s % 2:base + 512 * b + 256 * (s // 2 + 1):2] for s in range(4)], words[:, 512 * b:512 * (b + 1)], "s", nd[b])
+                if (kind, t) in dis:
+                    di = dis[(kind, t)]
+                    views = [di[:, (4 * b + s) * P:(4 * b + s + 1) * P] for s in range(4)]
+                else:
+                    w = xa_words(kind, t)
+                    views = [w[:, 256 * (2 * b + s // 2) + s % 2:256 * (2 * b + s // 2 + 1):2] for s in range(4)]
+                flip_bank(views, words[:, 512 * b:512 * (b + 1)], engs[b], nd[b])
 
         def q_xa(kind, t):
             codes, scales = (xc, xs) if kind == "x" else (ac, asc)
             nc.vector.quantize_mx(out=codes[:, t, :].bitcast(FP8X4), scales=scales[:, t, :], in_=grps[(kind, t)][:])
 
+        def d_w(c, d, engs="vv"):
+            di = dip.tile([P, 2048], F32, tag="di")
+            dis[("w", c, d)] = di
+            src = raws[("w", c, d)][:].bitcast(F32).rearrange("p (j k n u) -> p k j u n", j=4, k=2, u=2)
+            dst = di[:].rearrange("p (k j u n) -> p k j u n", k=2, j=4, u=2)
+            for k in range(2):
+                copy(engs[k], dst[:, k], src[:, k])
+
         def t_w(c, d, engs="ssss"):
             grp = grpp.tile([P, 4096], BF16, tag="grp", align_bytes=64)
             grps[("w", c, d)] = grp
-            w = raws[("w", c, d)][:].bitcast(F32)
             words = grp[:].bitcast(F32)
-            for k in range(2):
-                for b in range(2):
-                    views = [w[:, (2 * b + s // 2) * 512 + k * 256 + s % 2:(2 * b + s // 2) * 512 + (k + 1) * 256:2] for s in range(4)]
-                    flip_bank(views, words[:, 1024 * k + 512 * b:1024 * k + 512 * (b + 1)], engs[2 * k + b])
+            for b in range(4):
+                if ("w", c, d) in dis:
+                    di = dis[("w", c, d)]
+                    views = [di[:, (4 * b + s) * P:(4 * b + s + 1) * P] for s in range(4)]
+                else:
+                    w = raws[("w", c, d)][:].bitcast(F32)
+                    k = b // 2
+                    views = [w[:, (2 * (b % 2) + s // 2) * 512 + k * 256 + s % 2:(2 * (b % 2) + s // 2) * 512 + (k + 1) * 256:2] for s in range(4)]
+                flip_bank(views, words[:, 512 * b:512 * (b + 1)], engs[b])
 
-        def q_w(c, d):
-            wc = wcp.tile([P, 1024], U32, tag="wc", align_bytes=64)
-            ws = wcp.tile([P, 1024], U8, tag="ws", align_bytes=64)
-            wcs[(c, d)] = (wc, ws)
-            for k in range(2):
+        def q_w(c, d, ks=(0, 1)):
+            if ks[0] == 0:
+                wc = wcp.tile([P, 1024], U32, tag="wc", align_bytes=64)
+                ws = wcp.tile([P, 1024], U8, tag="ws", align_bytes=64)
+                wcs[(c, d)] = (wc, ws)
+            wc, ws = wcs[(c, d)]
+            for k in ks:
                 nc.vector.quantize_mx(
                     out=wc[:, k * 512:(k + 1) * 512].bitcast(FP8X4),
                     scales=ws[:, k * 512:(k + 1) * 512],
@@ -200,7 +224,6 @@ def tile_linearmoloralayer_pa_kernel(tc, x, gate_logits, W_base, b_base, A, B, o
                 a = accp.tile([P, 512], F32, tag="acc%d" % tt, name="acc%d" % tt)
                 tiles.append(a)
             accs[key] = tiles
-            return tiles
 
         def route_job():
             rw = rexp[:].rearrange("p t e i -> p t (e i)")
@@ -210,10 +233,9 @@ def tile_linearmoloralayer_pa_kernel(tc, x, gate_logits, W_base, b_base, A, B, o
             nc.scalar.copy(out=rt[:].rearrange("p t n -> p (t n)"), in_=st[:])
 
         def h_group(t, tt):
-            hps = accs["h"]
             for g in range(NG):
                 nc.tensor.matmul_mx(
-                    out=hps[tt][:, t * P:(t + 1) * P],
+                    out=accs["h"][tt][:, t * P:(t + 1) * P],
                     lhsT=ac[:, t, g * P:(g + 1) * P].bitcast(FP8X4),
                     lhsT_scale=asc[:, t, g * P:(g + 1) * P],
                     rhs=xc[:, tt, g * P:(g + 1) * P].bitcast(FP8X4),
@@ -233,46 +255,40 @@ def tile_linearmoloralayer_pa_kernel(tc, x, gate_logits, W_base, b_base, A, B, o
         def hw_quant():
             nc.vector.quantize_mx(out=hc[:].bitcast(FP8X4), scales=hsc[:], in_=hwg[:])
 
-        def shuffle_b(h):
+        def s_b(h, engs="vv"):
             src = raws[("b", h)][:].bitcast(F32).rearrange("p (e s v u) -> p u s e v", e=16, s=16, v=4)
             dst = bs[:].rearrange("p s u (e v) -> p u s e v", v=4)
             for u in range(2):
-                nc.vector.tensor_copy(out=dst[:, u, :, 16 * h:16 * h + 16, :], in_=src[:, u])
+                copy(engs[u], dst[:, u, :, 16 * h:16 * h + 16, :], src[:, u])
 
         def t_b(half, engs):
             bgw = bg[:].bitcast(F32).rearrange("p (n s u) -> p n s u", s=16, u=2)
-            for q in (2 * half, 2 * half + 1):
-                for b in range(2):
-                    st = stp.tile([P, 512], F32, tag="st")
-                    s0 = 4 * q + 2 * b
-                    for i in range(4):
-                        nc.tensor.transpose(st[:, i * P:(i + 1) * P], bs[:, s0 + i // 2, i % 2, :], ident[:])
-                    src = st[:].rearrange("p (s u n) -> p n s u", s=2, u=2)
-                    if engs[q % 2] == "v":
-                        nc.vector.tensor_copy(out=bgw[:, :, s0:s0 + 2, :], in_=src)
-                    else:
-                        nc.scalar.copy(out=bgw[:, :, s0:s0 + 2, :], in_=src)
+            for b in range(4):
+                st = stp.tile([P, 512], F32, tag="st")
+                s0 = 8 * half + 2 * b
+                for i in range(4):
+                    nc.tensor.transpose(st[:, i * P:(i + 1) * P], bs[:, s0 + i // 2, i % 2, :], ident[:])
+                copy(engs[b], bgw[:, :, s0:s0 + 2, :], st[:].rearrange("p (s u n) -> p n s u", s=2, u=2))
 
-        def q_b(hs):
-            for h in hs:
-                nc.vector.quantize_mx(
-                    out=bc[:, h * 1024:(h + 1) * 1024].bitcast(FP8X4),
-                    scales=bsc[:, h * 1024:(h + 1) * 1024],
-                    in_=bg[:, h * 4096:(h + 1) * 4096],
-                )
+        def q_b(c):
+            nc.vector.quantize_mx(
+                out=bc[:, c * 512:(c + 1) * 512].bitcast(FP8X4),
+                scales=bsc[:, c * 512:(c + 1) * 512],
+                in_=bg[:, c * 2048:(c + 1) * 2048],
+            )
 
-        def lora_pass(dst, c, tt, start, stop):
+        def lora_pass(c, tt, start=False):
             nc.tensor.matmul_mx(
-                out=dst[:],
+                out=accs[c][tt][:],
                 lhsT=hc[:, tt * P:(tt + 1) * P].bitcast(FP8X4),
                 lhsT_scale=hsc[:, tt * P:(tt + 1) * P],
                 rhs=bc[:, c * 512:(c + 1) * 512].bitcast(FP8X4),
                 rhs_scale=bsc[:, c * 512:(c + 1) * 512],
                 start=start,
-                stop=stop,
+                stop=True,
             )
 
-        def base_pass(c, g, tt, start, stop):
+        def base_pass(c, g, tt, stop=False):
             wc, ws = wcs[(c, g // 2)]
             k = g % 2
             nc.tensor.matmul_mx(
@@ -281,163 +297,130 @@ def tile_linearmoloralayer_pa_kernel(tc, x, gate_logits, W_base, b_base, A, B, o
                 lhsT_scale=xs[:, tt, g * P:(g + 1) * P],
                 rhs=wc[:, k * 512:(k + 1) * 512].bitcast(FP8X4),
                 rhs_scale=ws[:, k * 512:(k + 1) * 512],
-                start=start,
+                start=(g == 0),
                 stop=stop,
             )
-
-        def store(c, tt, src):
-            nc.sync.dma_start(out=of[tt * P:(tt + 1) * P, c * 512:(c + 1) * 512], in_=src)
 
         def p4(c, g):
             if g == 0:
                 new_acc(c)
             for tt in range(TT):
-                base_pass(c, g, tt, g == 0, False)
+                base_pass(c, g, tt)
 
         def evac(c, tt):
-            if c in DEFERRED:
-                dst = keep[:, DEFERRED.index(c) * TT + tt, :]
-            else:
-                osb = outp.tile([P, 512], F32, tag="osb")
-                dst = osb[:]
-            nc.vector.tensor_tensor(out=dst, in0=accs[c][tt][:], in1=bias_bc[:, c * 512:(c + 1) * 512], op=ALU.add)
-            if c not in DEFERRED:
-                store(c, tt, dst)
+            osb = outp.tile([P, 512], F32, tag="osb")
+            nc.vector.tensor_tensor(out=osb[:], in0=accs[c][tt][:], in1=bias_bc[:, c * 512:(c + 1) * 512], op=ALU.add)
+            nc.sync.dma_start(out=of[tt * P:(tt + 1) * P, c * 512:(c + 1) * 512], in_=osb[:])
 
-        def p_close(c, gs, tts):
-            late = c in DEFERRED
+        def p_keep(c, gs, tts):
             for tt in tts:
                 for g in gs:
-                    base_pass(c, g, tt, False, late and g == NG - 1)
-                if not late:
-                    lora_pass(accs[c][tt], c, tt, False, True)
+                    base_pass(c, g, tt, g == NG - 1)
+                nc.vector.tensor_tensor(out=keep[:, tt, :], in0=accs[c][tt][:], in1=bias_bc[:, c * 512:(c + 1) * 512], op=ALU.add)
+
+        def late_lora(c, tts, psum):
+            for tt in tts:
+                if psum == "acc":
+                    if tt == 0:
+                        new_acc(c)
+                else:
+                    st = stp.tile([P, 512], F32, tag="st")
+                    accs[c][tt] = st
+                lora_pass(c, tt, True)
+            for tt in tts:
+                osb = outp.tile([P, 512], F32, tag="osb")
+                nc.vector.tensor_tensor(out=osb[:], in0=accs[c][tt][:], in1=keep[:, tt, :], op=ALU.add)
+                nc.sync.dma_start(out=of[tt * P:(tt + 1) * P, c * 512:(c + 1) * 512], in_=osb[:])
+
+        def p_close(c, gs):
+            for tt in range(TT):
+                for g in gs:
+                    base_pass(c, g, tt)
+                lora_pass(c, tt)
                 evac(c, tt)
 
-        def p4_some(c, g, tts):
-            if g == 0:
-                new_acc(c)
-            for tt in tts:
-                base_pass(c, g, tt, g == 0, False)
-
-        def last_tile_in_halves(c, tt):
-            for half in range(2):
-                if half == 0:
-                    bank = accs[c][tt]
-                else:
-                    bank = stp.tile([P, 512], F32, tag="st", name="lasthalf")
-                cols = slice(c * 512 + half * 256, c * 512 + (half + 1) * 256)
-                for g in range(NG):
-                    wc, ws = wcs[(c, g // 2)]
-                    wcols = slice((g % 2) * 512 + half * 256, (g % 2) * 512 + (half + 1) * 256)
-                    nc.tensor.matmul_mx(
-                        out=bank[:, 0:256],
-                        lhsT=xc[:, tt, g * P:(g + 1) * P].bitcast(FP8X4),
-                        lhsT_scale=xs[:, tt, g * P:(g + 1) * P],
-                        rhs=wc[:, wcols].bitcast(FP8X4),
-                        rhs_scale=ws[:, wcols],
-                        start=(g == 0),
-                        stop=False,
-                    )
-                nc.tensor.matmul_mx(
-                    out=bank[:, 0:256],
-                    lhsT=hc[:, tt * P:(tt + 1) * P].bitcast(FP8X4),
-                    lhsT_scale=hsc[:, tt * P:(tt + 1) * P],
-                    rhs=bc[:, cols].bitcast(FP8X4),
-                    rhs_scale=bsc[:, cols],
-                    start=False,
-                    stop=True,
-                )
-                osb = outp.tile([P, 256], F32, tag="osb")
-                nc.vector.tensor_tensor(out=osb[:], in0=bank[:, 0:256], in1=bias_bc[:, cols], op=ALU.add)
-                nc.sync.dma_start(out=of[tt * P:(tt + 1) * P, cols], in_=osb[:])
-
-        def late_lora(c, where):
-            banks = []
+        def h_row(t, last=False):
             for tt in range(TT):
-                if where == "acc":
-                    a = accp.tile([P, 512], F32, tag="acc%d" % tt, name="late%d" % tt)
-                else:
-                    a = stp.tile([P, 512], F32, tag="st", name="late")
-                banks.append(a)
-                lora_pass(a, c, tt, True, True)
-            for tt in range(TT):
-                osb = outp.tile([P, 512], F32, tag="osb")
-                nc.vector.tensor_tensor(out=osb[:], in0=banks[tt][:], in1=keep[:, DEFERRED.index(c) * TT + tt, :], op=ALU.add)
-                store(c, tt, osb[:])
-
-        arr = []
-        for t in range(TT):
-            arr.append(("a", t))
-            arr.append(("x", t))
-        done = []
+                h_group(t, tt)
+                if last:
+                    hw_mult(tt)
         new_acc("h")
-        warm_up(5)
-        bias_job((0, 1, 2, 3))
-        for k in range(len(arr) + 2):
-            if k < len(arr):
-                t_xa(arr[k][0], arr[k][1], (1, 0) if k < 5 else (0, 0))
-            if k == 2:
-                softmax_head()
-            if k == 4:
-                softmax_tail()
-            if k == 5:
-                route_job()
-            if k == 8:
-                load_w(1, 1)
-                load_b(1)
-                load_w(2, 0)
-                load_w(2, 1)
-                t_w(0, 0)
-            if 1 <= k <= len(arr):
-                q_xa(arr[k - 1][0], arr[k - 1][1])
-            if k == 9:
-                q_w(0, 0)
-                t_w(0, 1)
-            if 2 <= k:
-                done.append(arr[k - 2])
-                for t2 in range(TT):
-                    for t1 in range(4):
-                        if ("a", t1) in done and ("x", t2) in done and (t1, t2) not in done:
-                            done.append((t1, t2))
-                            h_group(t1, t2)
-                            if t1 == 3:
-                                hw_mult(t2)
-
-        hw_quant()
+        warm_up(WARM)
+        t_xa("x", 0, (1, 0), "sv")
+        t_xa("x", 1, (1, 0), "sv")
+        q_xa("x", 0)
+        t_xa("x", 2, (1, 0), "sv")
+        q_xa("x", 1)
+        t_xa("x", 3, (1, 0), "ss")
+        q_xa("x", 2)
+        t_xa("a", 0, (1, 0))
+        softmax_head()
+        q_xa("x", 3)
+        t_xa("a", 1)
+        q_xa("a", 0)
+        softmax_tail()
+        h_row(0)
+        t_xa("a", 2)
+        q_xa("a", 1)
+        route_job()
+        h_row(1)
+        load_b(0)
+        load_b(1)
+        load_w(2, 0)
+        load_w(2, 1)
+        d_w(0, 0)
+        t_xa("a", 3)
+        q_xa("a", 2)
+        h_row(2)
+        t_w(0, 0)
+        q_xa("a", 3)
+        d_w(0, 1)
+        q_w(0, 0, (0,))
+        h_row(3, True)
+        q_w(0, 0, (1,))
+        d_w(1, 0)
+        t_w(0, 1)
         p4(0, 0)
         p4(0, 1)
         q_w(0, 1)
-        shuffle_b(0)
+        d_w(1, 1, "vs")
         t_w(1, 0)
         load_w(3, 0)
-        p_close(0, (2, 3), (0, 1))
-        q_w(1, 0)
-        p_close(0, (2, 3), (2, 3))
-        t_w(1, 1)
         load_w(3, 1)
-        shuffle_b(1)
+        p_keep(0, (2, 3), (0, 1, 2, 3))
+        q_w(1, 0)
+        d_w(2, 0, "vs")
+        t_w(1, 1)
         p4(1, 0)
-        q_w(1, 1)
-        t_b(0, "ss")
         p4(1, 1)
-        t_b(1, "sv")
+        s_b(0)
+        s_b(1, "vs")
+        hw_quant()
+        q_w(1, 1)
+        d_w(2, 1, "vs")
+        t_b(0, "ssvs")
         p4(1, 2)
-        t_w(2, 0)
-        q_b((0,))
+        t_b(1, "ssvs")
         p4(1, 3)
+        q_b(1)
+        q_b(0)
+        t_w(2, 0)
+        p_close(1, ())
         q_w(2, 0)
-        p_close(1, (), (0, 1, 2, 3))
+        d_w(3, 0, "vs")
+        q_b(2)
         t_w(2, 1)
-        late_lora(0, "acc")
-        q_w(2, 1)
-        t_w(3, 0)
-        q_b((1,))
+        late_lora(0, (0, 1, 2, 3), "acc")
         p4(2, 0)
         p4(2, 1)
+        q_w(2, 1)
+        d_w(3, 1, "vs")
+        t_w(3, 0)
+        p_close(2, (2, 3))
         q_w(3, 0)
         t_w(3, 1)
-        p_close(2, (2, 3), (0, 1, 2, 3))
-        q_w(3, 1)
+        q_b(3)
         p4(3, 0)
         p4(3, 1)
-        p_close(3, (2, 3), (0, 1, 2, 3))
+        q_w(3, 1)
+        p_close(3, (2, 3))

@@ -36,10 +36,10 @@ def tile_linearmoloralayer_pa_kernel(tc, x, gate_logits, W_base, b_base, A, B, o
     with ExitStack() as ctx:
         const = ctx.enter_context(tc.tile_pool(name="const", bufs=1))
         rawp = ctx.enter_context(tc.tile_pool(name="rawp", bufs=9))
-        dip = ctx.enter_context(tc.tile_pool(name="dip", bufs=3))
+        dip = ctx.enter_context(tc.tile_pool(name="dip", bufs=4))
         grpp = ctx.enter_context(tc.tile_pool(name="grpp", bufs=3))
         wcp = ctx.enter_context(tc.tile_pool(name="wcp", bufs=3))
-        outp = ctx.enter_context(tc.tile_pool(name="outp", bufs=4))
+        outp = ctx.enter_context(tc.tile_pool(name="outp", bufs=8))
         accp = ctx.enter_context(tc.psum_pool(name="accp", bufs=1))
         stp = ctx.enter_context(tc.psum_pool(name="stp", bufs=4))
         ctx.enter_context(tc.manual_schedule())
@@ -75,6 +75,8 @@ def tile_linearmoloralayer_pa_kernel(tc, x, gate_logits, W_base, b_base, A, B, o
 
         ident = const.tile([P, P], F32)
         make_identity(nc, ident[:])
+        brow = const.tile([P, 512], BF16)
+        nc.vector.memset(brow[:].bitcast(I32), 0)
         zeros = const.tile([P, 512], BF16)
         nc.vector.memset(zeros[:].bitcast(I32), 0)
         ones = const.tile([P, P], BF16)
@@ -83,20 +85,20 @@ def tile_linearmoloralayer_pa_kernel(tc, x, gate_logits, W_base, b_base, A, B, o
         nc.vector.memset(warm[:], 0.0)
         nc.scalar.activation(out=warm[:], in_=warm[:], func=ACT.Exp)
 
+        identb = const.tile([P, P], BF16)
+        nc.vector.tensor_copy(out=identb[:], in_=ident[:])
+        nc.sync.dma_start(out=brow[0:NC, :], in_=b_base.rearrange("(c n) -> c n", c=NC))
         gl = const.tile([P, TT, E], BF16)
+        nc.sync.dma_start(out=gl[:], in_=gf.rearrange("(t p) e -> p t e", p=P))
         for t in range(TT):
             raw_xa(t)
             load_x(t)
-            if t == 0:
-                nc.sync.dma_start(out=gl[:], in_=gf.rearrange("(t p) e -> p t e", p=P))
         for t in range(TT):
             load_a(t)
         load_w(0, 0)
         load_w(0, 1)
-        bias_bc = const.tile([P, O], BF16)
-        nc.sync.dma_start(out=bias_bc[:], in_=b_base.partition_broadcast(P))
         load_w(1, 0)
-        load_w(1, 1)
+        load_b(0)
 
         xc = const.tile([P, TT, 512], U32, align_bytes=64)
         xs = const.tile([P, TT, 512], U8, align_bytes=64)
@@ -108,11 +110,11 @@ def tile_linearmoloralayer_pa_kernel(tc, x, gate_logits, W_base, b_base, A, B, o
         hsc = const.tile([P, 512], U8, align_bytes=64)
         hwg = const.tile([P, 2048], BF16, align_bytes=64)
         bg = const.tile([P, 4 * O], BF16, align_bytes=64)
-        bs = const.tile([P, 16, 2, P], F32)
         rt = const.tile([P, TT, P], F32)
         rexp = const.tile([P, TT, E, 4], F32)
         ex = const.tile([P, TT, E], F32)
         keep = const.tile([P, TT, 512], F32)
+        bias_bc = const.tile([P, O], F32)
 
         def copy(eng, out_ap, in_ap):
             if eng == "v":
@@ -148,6 +150,12 @@ def tile_linearmoloralayer_pa_kernel(tc, x, gate_logits, W_base, b_base, A, B, o
             st = stp.tile([P, 512], F32, tag="st")
             for i in range(n):
                 dummy(st)
+
+        def bias_job():
+            for c in range(NC):
+                st = stp.tile([P, 512], F32, tag="st")
+                nc.tensor.matmul(out=st[:], lhsT=identb[:, c:c + 1].to_broadcast([P, P]), rhs=brow[:], start=True, stop=True)
+                copy("vs"[c % 2], bias_bc[:, c * 512:(c + 1) * 512], st[:])
 
         def flip_bank(views, words, eng, ndummy=0):
             st = stp.tile([P, 512], F32, tag="st")
@@ -257,9 +265,13 @@ def tile_linearmoloralayer_pa_kernel(tc, x, gate_logits, W_base, b_base, A, B, o
 
         def s_b(h, engs="vv"):
             src = raws[("b", h)][:].bitcast(F32).rearrange("p (e s v u) -> p u s e v", e=16, s=16, v=4)
-            dst = bs[:].rearrange("p s u (e v) -> p u s e v", v=4)
-            for u in range(2):
-                copy(engs[u], dst[:, u, :, 16 * h:16 * h + 16, :], src[:, u])
+            for half in range(2):
+                if h == 0:
+                    di = dip.tile([P, 2048], F32, tag="di")
+                    dis[("b", half)] = di
+                dst = dis[("b", half)][:].rearrange("p (s u e v) -> p u s e v", s=8, u=2, v=4)
+                for u in range(2):
+                    copy(engs[half], dst[:, u, :, 16 * h:16 * h + 16, :], src[:, u, 8 * half:8 * half + 8])
 
         def t_b(half, engs):
             bgw = bg[:].bitcast(F32).rearrange("p (n s u) -> p n s u", s=16, u=2)
@@ -267,7 +279,8 @@ def tile_linearmoloralayer_pa_kernel(tc, x, gate_logits, W_base, b_base, A, B, o
                 st = stp.tile([P, 512], F32, tag="st")
                 s0 = 8 * half + 2 * b
                 for i in range(4):
-                    nc.tensor.transpose(st[:, i * P:(i + 1) * P], bs[:, s0 + i // 2, i % 2, :], ident[:])
+                    col = (2 * (2 * b + i // 2) + i % 2) * P
+                    nc.tensor.transpose(st[:, i * P:(i + 1) * P], dis[("b", half)][:, col:col + P], ident[:])
                 copy(engs[b], bgw[:, :, s0:s0 + 2, :], st[:].rearrange("p (s u n) -> p n s u", s=2, u=2))
 
         def q_b(c):
@@ -312,11 +325,13 @@ def tile_linearmoloralayer_pa_kernel(tc, x, gate_logits, W_base, b_base, A, B, o
             nc.vector.tensor_tensor(out=osb[:], in0=accs[c][tt][:], in1=bias_bc[:, c * 512:(c + 1) * 512], op=ALU.add)
             nc.sync.dma_start(out=of[tt * P:(tt + 1) * P, c * 512:(c + 1) * 512], in_=osb[:])
 
-        def p_keep(c, gs, tts):
+        def p_keep(c, gs, tts, then=()):
             for tt in tts:
                 for g in gs:
                     base_pass(c, g, tt, g == NG - 1)
                 nc.vector.tensor_tensor(out=keep[:, tt, :], in0=accs[c][tt][:], in1=bias_bc[:, c * 512:(c + 1) * 512], op=ALU.add)
+                if tt < len(then):
+                    then[tt]()
 
         def late_lora(c, tts, psum):
             for tt in tts:
@@ -332,12 +347,14 @@ def tile_linearmoloralayer_pa_kernel(tc, x, gate_logits, W_base, b_base, A, B, o
                 nc.vector.tensor_tensor(out=osb[:], in0=accs[c][tt][:], in1=keep[:, tt, :], op=ALU.add)
                 nc.sync.dma_start(out=of[tt * P:(tt + 1) * P, c * 512:(c + 1) * 512], in_=osb[:])
 
-        def p_close(c, gs):
+        def p_close(c, gs, then=()):
             for tt in range(TT):
                 for g in gs:
                     base_pass(c, g, tt)
                 lora_pass(c, tt)
                 evac(c, tt)
+                if tt < len(then):
+                    then[tt]()
 
         def h_row(t, last=False):
             for tt in range(TT):
@@ -346,39 +363,42 @@ def tile_linearmoloralayer_pa_kernel(tc, x, gate_logits, W_base, b_base, A, B, o
                     hw_mult(tt)
         new_acc("h")
         warm_up(WARM)
+        bias_job()
+        softmax_head()
+        softmax_tail()
         t_xa("x", 0, (1, 0), "sv")
         t_xa("x", 1, (1, 0), "sv")
         q_xa("x", 0)
         t_xa("x", 2, (1, 0), "sv")
         q_xa("x", 1)
-        t_xa("x", 3, (1, 0), "ss")
+        t_xa("x", 3, (1, 0), "sv")
         q_xa("x", 2)
         t_xa("a", 0, (1, 0))
-        softmax_head()
         q_xa("x", 3)
         t_xa("a", 1)
+        d_xa("a", 2)
         q_xa("a", 0)
-        softmax_tail()
-        h_row(0)
-        t_xa("a", 2)
+        t_xa("a", 2, (0, 0), "ss")
+        d_xa("a", 3)
         q_xa("a", 1)
+        h_row(0)
         route_job()
-        h_row(1)
-        load_b(0)
+        t_xa("a", 3, (0, 0), "ss")
+        d_w(0, 0)
+        load_w(1, 1)
         load_b(1)
         load_w(2, 0)
         load_w(2, 1)
-        d_w(0, 0)
-        t_xa("a", 3)
         q_xa("a", 2)
-        h_row(2)
+        h_row(1)
         t_w(0, 0)
-        q_xa("a", 3)
         d_w(0, 1)
+        q_xa("a", 3)
+        h_row(2)
         q_w(0, 0, (0,))
         h_row(3, True)
         q_w(0, 0, (1,))
-        d_w(1, 0)
+        d_w(1, 0, "vs")
         t_w(0, 1)
         p4(0, 0)
         p4(0, 1)
@@ -387,13 +407,13 @@ def tile_linearmoloralayer_pa_kernel(tc, x, gate_logits, W_base, b_base, A, B, o
         t_w(1, 0)
         load_w(3, 0)
         load_w(3, 1)
-        p_keep(0, (2, 3), (0, 1, 2, 3))
-        q_w(1, 0)
+        s_b(0)
+        p_keep(0, (2, 3), (0, 1, 2, 3), (lambda: None, lambda: q_w(1, 0, (0,))))
+        q_w(1, 0, (1,))
         d_w(2, 0, "vs")
         t_w(1, 1)
         p4(1, 0)
         p4(1, 1)
-        s_b(0)
         s_b(1, "vs")
         hw_quant()
         q_w(1, 1)
@@ -403,24 +423,24 @@ def tile_linearmoloralayer_pa_kernel(tc, x, gate_logits, W_base, b_base, A, B, o
         t_b(1, "ssvs")
         p4(1, 3)
         q_b(1)
-        q_b(0)
         t_w(2, 0)
-        p_close(1, ())
-        q_w(2, 0)
+        p_close(1, (), (lambda: None, lambda: q_w(2, 0, (0,))))
+        q_w(2, 0, (1,))
         d_w(3, 0, "vs")
         q_b(2)
         t_w(2, 1)
-        late_lora(0, (0, 1, 2, 3), "acc")
         p4(2, 0)
         p4(2, 1)
         q_w(2, 1)
         d_w(3, 1, "vs")
         t_w(3, 0)
-        p_close(2, (2, 3))
-        q_w(3, 0)
-        t_w(3, 1)
+        p_close(2, (2, 3), (lambda: None, lambda: q_w(3, 0, (0,))))
+        q_w(3, 0, (1,))
         q_b(3)
+        q_b(0)
+        t_w(3, 1)
         p4(3, 0)
         p4(3, 1)
         q_w(3, 1)
+        late_lora(0, (0, 1, 2, 3), "st")
         p_close(3, (2, 3))

@@ -172,7 +172,7 @@ def tile_linearmoloralayer_pa_kernel(tc, x, gate_logits, W_base, b_base, A, B, o
         def d_xa(kind, t, eng="v"):
             di = dip.tile([P, 2048], F32, tag="di")
             dis[(kind, t)] = di
-            copy(eng, di[:, 0:1024].rearrange("p (g u n) -> p g u n", g=4, u=2), xa_words(kind, t).rearrange("p (g n u) -> p g u n", g=4, u=2))
+            copy(eng, di[:, 0:1024].rearrange("p (g u n) -> p g n u", g=4, u=2), xa_words(kind, t).rearrange("p (g n u) -> p g n u", g=4, u=2))
 
         def t_xa(kind, t, nd=(0, 0), engs="ss"):
             grp = grpp.tile([P, 2048], BF16, tag="grp", align_bytes=64)
@@ -194,8 +194,8 @@ def tile_linearmoloralayer_pa_kernel(tc, x, gate_logits, W_base, b_base, A, B, o
         def d_w(c, d, engs="vv"):
             di = dip.tile([P, 2048], F32, tag="di")
             dis[("w", c, d)] = di
-            src = raws[("w", c, d)][:].bitcast(F32).rearrange("p (j k n u) -> p k j u n", j=4, k=2, u=2)
-            dst = di[:].rearrange("p (k j u n) -> p k j u n", k=2, j=4, u=2)
+            src = raws[("w", c, d)][:].bitcast(F32).rearrange("p (j k n u) -> p k j n u", j=4, k=2, u=2)
+            dst = di[:].rearrange("p (k j u n) -> p k j n u", k=2, j=4, u=2)
             for k in range(2):
                 copy(engs[k], dst[:, k], src[:, k])
 
@@ -264,14 +264,13 @@ def tile_linearmoloralayer_pa_kernel(tc, x, gate_logits, W_base, b_base, A, B, o
             nc.vector.quantize_mx(out=hc[:].bitcast(FP8X4), scales=hsc[:], in_=hwg[:])
 
         def s_b(h, engs="vv"):
-            src = raws[("b", h)][:].bitcast(F32).rearrange("p (e s v u) -> p u s e v", e=16, s=16, v=4)
+            src = raws[("b", h)][:].bitcast(F32).rearrange("p (e s v u) -> p s e v u", e=16, s=16, v=4)
             for half in range(2):
                 if h == 0:
                     di = dip.tile([P, 2048], F32, tag="di")
                     dis[("b", half)] = di
-                dst = dis[("b", half)][:].rearrange("p (s u e v) -> p u s e v", s=8, u=2, v=4)
-                for u in range(2):
-                    copy(engs[half], dst[:, u, :, 16 * h:16 * h + 16, :], src[:, u, 8 * half:8 * half + 8])
+                dst = dis[("b", half)][:].rearrange("p (s u e v) -> p s e v u", s=8, u=2, v=4)
+                copy(engs[half], dst[:, :, 16 * h:16 * h + 16], src[:, 8 * half:8 * half + 8])
 
         def t_b(half, engs):
             bgw = bg[:].bitcast(F32).rearrange("p (n s u) -> p n s u", s=16, u=2)

@@ -23,6 +23,7 @@ NG = 4
 NC = 4
 FLOPS = 2 * 512 * D * O + 2 * 512 * D * 512 + 2 * 512 * 512 * O
 WARM = 3
+NKEEP = 3
 
 
 def tile_linearmoloralayer_pa_kernel(tc, x, gate_logits, W_base, b_base, A, B, out):
@@ -39,8 +40,8 @@ def tile_linearmoloralayer_pa_kernel(tc, x, gate_logits, W_base, b_base, A, B, o
         dip = ctx.enter_context(tc.tile_pool(name="dip", bufs=4))
         grpp = ctx.enter_context(tc.tile_pool(name="grpp", bufs=3))
         wcp = ctx.enter_context(tc.tile_pool(name="wcp", bufs=3))
-        outp = ctx.enter_context(tc.tile_pool(name="outp", bufs=8))
-        accp = ctx.enter_context(tc.psum_pool(name="accp", bufs=1))
+        outp = ctx.enter_context(tc.tile_pool(name="outp", bufs=6))
+        accp = ctx.enter_context(tc.psum_pool(name="accp", bufs=4))
         stp = ctx.enter_context(tc.psum_pool(name="stp", bufs=4))
         ctx.enter_context(tc.manual_schedule())
 
@@ -60,13 +61,10 @@ def tile_linearmoloralayer_pa_kernel(tc, x, gate_logits, W_base, b_base, A, B, o
             r = rawp.tile([P, 4096], BF16, tag="raw")
             raws[("xa", t)] = r
 
-        def load_w(c, d):
+        def load_w(s):
             r = rawp.tile([P, 4096], BF16, tag="raw")
-            nc.sync.dma_start(
-                out=r[:].rearrange("p (j k) -> p j k", j=4),
-                in_=W_base[c * 512:(c + 1) * 512, d * 1024:(d + 1) * 1024].rearrange("(j p) k -> p j k", p=P),
-            )
-            raws[("w", c, d)] = r
+            nc.sync.dma_start(out=r[:], in_=W_base[s * 256:(s + 1) * 256, :].rearrange("(p j) k -> p (j k)", j=2))
+            raws[("w", s)] = r
 
         def load_b(h):
             r = rawp.tile([P, 4096], BF16, tag="raw")
@@ -95,9 +93,9 @@ def tile_linearmoloralayer_pa_kernel(tc, x, gate_logits, W_base, b_base, A, B, o
             load_x(t)
         for t in range(TT):
             load_a(t)
-        load_w(0, 0)
-        load_w(0, 1)
-        load_w(1, 0)
+        load_w(0)
+        load_w(1)
+        load_w(2)
         load_b(0)
 
         xc = const.tile([P, TT, 512], U32, align_bytes=64)
@@ -113,7 +111,7 @@ def tile_linearmoloralayer_pa_kernel(tc, x, gate_logits, W_base, b_base, A, B, o
         rt = const.tile([P, TT, P], F32)
         rexp = const.tile([P, TT, E, 4], F32)
         ex = const.tile([P, TT, E], F32)
-        keep = const.tile([P, TT, 512], F32)
+        keep = const.tile([P, 2 * NKEEP, 2, 256], F32)
         bias_bc = const.tile([P, O], F32)
 
         def copy(eng, out_ap, in_ap):
@@ -191,45 +189,47 @@ def tile_linearmoloralayer_pa_kernel(tc, x, gate_logits, W_base, b_base, A, B, o
             codes, scales = (xc, xs) if kind == "x" else (ac, asc)
             nc.vector.quantize_mx(out=codes[:, t, :].bitcast(FP8X4), scales=scales[:, t, :], in_=grps[(kind, t)][:])
 
-        def d_w(c, d, engs="vv"):
+        def d_w(s, engs="vv"):
             di = dip.tile([P, 2048], F32, tag="di")
-            dis[("w", c, d)] = di
-            src = raws[("w", c, d)][:].bitcast(F32).rearrange("p (j k n u) -> p k j n u", j=4, k=2, u=2)
-            dst = di[:].rearrange("p (k j u n) -> p k j n u", k=2, j=4, u=2)
-            for k in range(2):
-                copy(engs[k], dst[:, k], src[:, k])
+            dis[("w", s)] = di
+            src = raws[("w", s)][:].bitcast(F32).rearrange("p (j g n u) -> p g j n u", j=2, g=4, u=2)
+            dst = di[:].rearrange("p (g j u n) -> p g j n u", g=4, j=2, u=2)
+            for h in range(2):
+                copy(engs[h], dst[:, 2 * h:2 * h + 2], src[:, 2 * h:2 * h + 2])
 
-        def t_w(c, d, engs="ssss"):
+        def t_w(s, engs="ssss"):
             grp = grpp.tile([P, 4096], BF16, tag="grp", align_bytes=64)
-            grps[("w", c, d)] = grp
+            grps[("w", s)] = grp
             words = grp[:].bitcast(F32)
-            for b in range(4):
-                if ("w", c, d) in dis:
-                    di = dis[("w", c, d)]
-                    views = [di[:, (4 * b + s) * P:(4 * b + s + 1) * P] for s in range(4)]
-                else:
-                    w = raws[("w", c, d)][:].bitcast(F32)
-                    k = b // 2
-                    views = [w[:, (2 * (b % 2) + s // 2) * 512 + k * 256 + s % 2:(2 * (b % 2) + s // 2) * 512 + (k + 1) * 256:2] for s in range(4)]
-                flip_bank(views, words[:, 512 * b:512 * (b + 1)], engs[b])
+            for g in range(NG):
+                st = stp.tile([P, 512], F32, tag="st")
+                for j in range(2):
+                    for u in range(2):
+                        i = 2 * j + u
+                        if ("w", s) in dis:
+                            view = dis[("w", s)][:, (4 * g + i) * P:(4 * g + i + 1) * P]
+                        else:
+                            view = raws[("w", s)][:].bitcast(F32)[:, j * 1024 + g * 256 + u:j * 1024 + (g + 1) * 256:2]
+                        nc.tensor.transpose(st[:, i * P:(i + 1) * P], view, ident[:])
+                copy(engs[g], words[:, 512 * g:512 * (g + 1)].rearrange("p (n j u) -> p n j u", j=2, u=2), st[:].rearrange("p (j u n) -> p n j u", j=2, u=2))
 
-        def q_w(c, d, ks=(0, 1)):
+        def q_w(s, ks=(0, 1)):
             if ks[0] == 0:
                 wc = wcp.tile([P, 1024], U32, tag="wc", align_bytes=64)
                 ws = wcp.tile([P, 1024], U8, tag="ws", align_bytes=64)
-                wcs[(c, d)] = (wc, ws)
-            wc, ws = wcs[(c, d)]
+                wcs[s] = (wc, ws)
+            wc, ws = wcs[s]
             for k in ks:
                 nc.vector.quantize_mx(
                     out=wc[:, k * 512:(k + 1) * 512].bitcast(FP8X4),
                     scales=ws[:, k * 512:(k + 1) * 512],
-                    in_=grps[("w", c, d)][:, k * 2048:(k + 1) * 2048],
+                    in_=grps[("w", s)][:, k * 2048:(k + 1) * 2048],
                 )
 
         def new_acc(key):
             tiles = []
             for tt in range(TT):
-                a = accp.tile([P, 512], F32, tag="acc%d" % tt, name="acc%d" % tt)
+                a = accp.tile([P, 512], F32, tag="acc", name="acc")
                 tiles.append(a)
             accs[key] = tiles
 
@@ -289,71 +289,74 @@ def tile_linearmoloralayer_pa_kernel(tc, x, gate_logits, W_base, b_base, A, B, o
                 in_=bg[:, c * 2048:(c + 1) * 2048],
             )
 
-        def lora_pass(c, tt, start=False):
+        def half_bank(bank, tt):
+            return bank[:, (tt % 2) * 256:(tt % 2 + 1) * 256]
+
+        def lora_pass(bank, s, tt, start):
             nc.tensor.matmul_mx(
-                out=accs[c][tt][:],
+                out=half_bank(bank, tt),
                 lhsT=hc[:, tt * P:(tt + 1) * P].bitcast(FP8X4),
                 lhsT_scale=hsc[:, tt * P:(tt + 1) * P],
-                rhs=bc[:, c * 512:(c + 1) * 512].bitcast(FP8X4),
-                rhs_scale=bsc[:, c * 512:(c + 1) * 512],
+                rhs=bc[:, s * 256:(s + 1) * 256].bitcast(FP8X4),
+                rhs_scale=bsc[:, s * 256:(s + 1) * 256],
                 start=start,
                 stop=True,
             )
 
-        def base_pass(c, g, tt, stop=False):
-            wc, ws = wcs[(c, g // 2)]
-            k = g % 2
-            nc.tensor.matmul_mx(
-                out=accs[c][tt][:],
-                lhsT=xc[:, tt, g * P:(g + 1) * P].bitcast(FP8X4),
-                lhsT_scale=xs[:, tt, g * P:(g + 1) * P],
-                rhs=wc[:, k * 512:(k + 1) * 512].bitcast(FP8X4),
-                rhs_scale=ws[:, k * 512:(k + 1) * 512],
-                start=(g == 0),
-                stop=stop,
+        def p_slab(s, b, lora=True, each=None):
+            bank = accp.tile([P, 512], F32, tag="acc", name="acc")
+            accs[(s, b)] = bank
+            wc, ws = wcs[s]
+            for tt in (2 * b, 2 * b + 1):
+                for g in range(NG):
+                    nc.tensor.matmul_mx(
+                        out=half_bank(bank, tt),
+                        lhsT=xc[:, tt, g * P:(g + 1) * P].bitcast(FP8X4),
+                        lhsT_scale=xs[:, tt, g * P:(g + 1) * P],
+                        rhs=wc[:, g * 256:(g + 1) * 256].bitcast(FP8X4),
+                        rhs_scale=ws[:, g * 256:(g + 1) * 256],
+                        start=(g == 0),
+                        stop=(g == NG - 1 and not lora),
+                    )
+                if lora:
+                    lora_pass(bank, s, tt, False)
+                if each:
+                    each(s, tt)
+
+        def pair(bank):
+            return bank[:].rearrange("p (t n) -> p t n", t=2)
+
+        def store(s, b, osb):
+            nc.sync.dma_start(
+                out=of[2 * b * P:(2 * b + 2) * P, s * 256:(s + 1) * 256].rearrange("(t p) n -> p t n", p=P),
+                in_=osb[:],
             )
 
-        def p4(c, g):
-            if g == 0:
-                new_acc(c)
-            for tt in range(TT):
-                base_pass(c, g, tt)
+        def evac(s, b):
+            bias = bias_bc[:, s * 256:(s + 1) * 256].unsqueeze(1).to_broadcast([P, 2, 256])
+            if s < NKEEP:
+                nc.vector.tensor_tensor(out=keep[:, 2 * s + b, :, :], in0=pair(accs[(s, b)]), in1=bias, op=ALU.add)
+            else:
+                osb = outp.tile([P, 2, 256], F32, tag="osb")
+                nc.vector.tensor_tensor(out=osb[:], in0=pair(accs[(s, b)]), in1=bias, op=ALU.add)
+                store(s, b, osb)
 
-        def evac(c, tt):
-            osb = outp.tile([P, 512], F32, tag="osb")
-            nc.vector.tensor_tensor(out=osb[:], in0=accs[c][tt][:], in1=bias_bc[:, c * 512:(c + 1) * 512], op=ALU.add)
-            nc.sync.dma_start(out=of[tt * P:(tt + 1) * P, c * 512:(c + 1) * 512], in_=osb[:])
+        def evac_one(s, tt):
+            osb = outp.tile([P, 256], F32, tag="osb")
+            cols = slice(s * 256, (s + 1) * 256)
+            nc.vector.tensor_tensor(out=osb[:], in0=half_bank(accs[(s, tt // 2)], tt), in1=bias_bc[:, cols], op=ALU.add)
+            nc.sync.dma_start(out=of[tt * P:(tt + 1) * P, cols], in_=osb[:])
 
-        def p_keep(c, gs, tts, then=()):
-            for tt in tts:
-                for g in gs:
-                    base_pass(c, g, tt, g == NG - 1)
-                nc.vector.tensor_tensor(out=keep[:, tt, :], in0=accs[c][tt][:], in1=bias_bc[:, c * 512:(c + 1) * 512], op=ALU.add)
-                if tt < len(then):
-                    then[tt]()
+        def late_pass(s, b):
+            bank = accp.tile([P, 512], F32, tag="acc", name="acc")
+            accs[(s, b)] = bank
+            for tt in (2 * b, 2 * b + 1):
+                lora_pass(bank, s, tt, True)
 
-        def late_lora(c, tts, psum):
-            for tt in tts:
-                if psum == "acc":
-                    if tt == 0:
-                        new_acc(c)
-                else:
-                    st = stp.tile([P, 512], F32, tag="st")
-                    accs[c][tt] = st
-                lora_pass(c, tt, True)
-            for tt in tts:
-                osb = outp.tile([P, 512], F32, tag="osb")
-                nc.vector.tensor_tensor(out=osb[:], in0=accs[c][tt][:], in1=keep[:, tt, :], op=ALU.add)
-                nc.sync.dma_start(out=of[tt * P:(tt + 1) * P, c * 512:(c + 1) * 512], in_=osb[:])
-
-        def p_close(c, gs, then=()):
-            for tt in range(TT):
-                for g in gs:
-                    base_pass(c, g, tt)
-                lora_pass(c, tt)
-                evac(c, tt)
-                if tt < len(then):
-                    then[tt]()
+        def late_add(s, b):
+            osb = outp.tile([P, 2, 256], F32, tag="osb")
+            nc.vector.tensor_tensor(out=osb[:], in0=pair(accs[(s, b)]), in1=keep[:, 2 * s + b, :, :], op=ALU.add)
+            store(s, b, osb)
 
         def h_row(t, last=False):
             for tt in range(TT):
@@ -365,12 +368,12 @@ def tile_linearmoloralayer_pa_kernel(tc, x, gate_logits, W_base, b_base, A, B, o
         bias_job()
         softmax_head()
         softmax_tail()
-        t_xa("x", 0, (1, 0), "sv")
-        t_xa("x", 1, (1, 0), "sv")
+        t_xa("x", 0, (1, 0), "ss")
+        t_xa("x", 1, (1, 0), "ss")
         q_xa("x", 0)
-        t_xa("x", 2, (1, 0), "sv")
+        t_xa("x", 2, (1, 0), "ss")
         q_xa("x", 1)
-        t_xa("x", 3, (1, 0), "sv")
+        t_xa("x", 3, (1, 0), "ss")
         q_xa("x", 2)
         t_xa("a", 0, (1, 0))
         q_xa("x", 3)
@@ -383,63 +386,96 @@ def tile_linearmoloralayer_pa_kernel(tc, x, gate_logits, W_base, b_base, A, B, o
         h_row(0)
         route_job()
         t_xa("a", 3, (0, 0), "ss")
-        d_w(0, 0)
-        load_w(1, 1)
+        d_w(0)
+        load_w(3)
         load_b(1)
-        load_w(2, 0)
-        load_w(2, 1)
+        load_w(4)
+        load_w(5)
         q_xa("a", 2)
         h_row(1)
-        t_w(0, 0)
-        d_w(0, 1)
+        t_w(0)
+        d_w(1)
         q_xa("a", 3)
         h_row(2)
-        q_w(0, 0, (0,))
+        q_w(0)
         h_row(3, True)
-        q_w(0, 0, (1,))
-        d_w(1, 0, "vs")
-        t_w(0, 1)
-        p4(0, 0)
-        p4(0, 1)
-        q_w(0, 1)
-        d_w(1, 1, "vs")
-        t_w(1, 0)
-        load_w(3, 0)
-        load_w(3, 1)
-        s_b(0)
-        p_keep(0, (2, 3), (0, 1, 2, 3), (lambda: None, lambda: q_w(1, 0, (0,))))
-        q_w(1, 0, (1,))
-        d_w(2, 0, "vs")
-        t_w(1, 1)
-        p4(1, 0)
-        p4(1, 1)
+        d_w(2, "vs")
+        t_w(1)
+        p_slab(0, 0, False)
+        q_w(1, (0,))
+        evac(0, 0)
+        q_w(1, (1,))
+        p_slab(0, 1, False)
+        evac(0, 1)
+        load_w(6)
+        t_w(2)
+        p_slab(1, 0, False)
+        s_b(0, "vs")
+        d_w(3, "vv")
+        q_w(2, (0,))
+        evac(1, 0)
+        q_w(2, (1,))
+        p_slab(1, 1, False)
+        evac(1, 1)
+        load_w(7)
         s_b(1, "vs")
+        t_w(3)
         hw_quant()
-        q_w(1, 1)
-        d_w(2, 1, "vs")
+        p_slab(2, 0, False)
+        evac(2, 0)
+        q_w(3)
         t_b(0, "ssvs")
-        p4(1, 2)
-        t_b(1, "ssvs")
-        p4(1, 3)
+        p_slab(2, 1, False)
+        evac(2, 1)
+        d_w(4, "vv")
+        t_b(1, "svsv")
         q_b(1)
-        t_w(2, 0)
-        p_close(1, (), (lambda: None, lambda: q_w(2, 0, (0,))))
-        q_w(2, 0, (1,))
-        d_w(3, 0, "vs")
+        d_w(5, "vs")
+        t_w(4)
+        p_slab(3, 0)
+        q_w(4, (0,))
+        evac(3, 0)
+        q_w(4, (1,))
+        p_slab(3, 1)
+        evac(3, 1)
+        d_w(6, "vs")
+        t_w(5)
         q_b(2)
-        t_w(2, 1)
-        p4(2, 0)
-        p4(2, 1)
-        q_w(2, 1)
-        d_w(3, 1, "vs")
-        t_w(3, 0)
-        p_close(2, (2, 3), (lambda: None, lambda: q_w(3, 0, (0,))))
-        q_w(3, 0, (1,))
-        q_b(3)
+        p_slab(4, 0)
+        q_w(5, (0,))
         q_b(0)
-        t_w(3, 1)
-        p4(3, 0)
-        p4(3, 1)
-        q_w(3, 1)
-        late_lora(0, (0, 1, 2, 3), "st")
-        p_close(3, (2, 3))
+        evac(4, 0)
+        q_w(5, (1,))
+        p_slab(4, 1)
+        evac(4, 1)
+        late_pass(0, 0)
+        late_add(0, 0)
+        late_pass(0, 1)
+        late_add(0, 1)
+        d_w(7, "vs")
+        t_w(6)
+        p_slab(5, 0)
+        q_w(6, (0,))
+        evac(5, 0)
+        q_w(6, (1,))
+        p_slab(5, 1)
+        evac(5, 1)
+        q_b(3)
+        late_pass(1, 0)
+        late_add(1, 0)
+        late_pass(1, 1)
+        late_add(1, 1)
+        t_w(7)
+        p_slab(6, 0)
+        q_w(7, (0,))
+        evac(6, 0)
+        q_w(7, (1,))
+        p_slab(6, 1)
+        evac(6, 1)
+        late_pass(2, 0)
+        late_add(2, 0)
+        late_pass(2, 1)
+        late_add(2, 1)
+        p_slab(7, 0)
+        evac(7, 0)
+        p_slab(7, 1, True, evac_one)

@@ -23,7 +23,6 @@ NG = 4
 NC = 4
 FLOPS = 2 * 512 * D * O + 2 * 512 * D * 512 + 2 * 512 * 512 * O
 WARM = 3
-NKEEP = 3
 
 
 def tile_linearmoloralayer_pa_kernel(tc, x, gate_logits, W_base, b_base, A, B, out):
@@ -36,11 +35,11 @@ def tile_linearmoloralayer_pa_kernel(tc, x, gate_logits, W_base, b_base, A, B, o
 
     with ExitStack() as ctx:
         const = ctx.enter_context(tc.tile_pool(name="const", bufs=1))
-        rawp = ctx.enter_context(tc.tile_pool(name="rawp", bufs=9))
+        rawp = ctx.enter_context(tc.tile_pool(name="rawp", bufs=8))
         dip = ctx.enter_context(tc.tile_pool(name="dip", bufs=4))
         grpp = ctx.enter_context(tc.tile_pool(name="grpp", bufs=3))
-        wcp = ctx.enter_context(tc.tile_pool(name="wcp", bufs=3))
-        outp = ctx.enter_context(tc.tile_pool(name="outp", bufs=6))
+        wcp = ctx.enter_context(tc.tile_pool(name="wcp", bufs=2))
+        outp = ctx.enter_context(tc.tile_pool(name="outp", bufs=4))
         accp = ctx.enter_context(tc.psum_pool(name="accp", bufs=4))
         stp = ctx.enter_context(tc.psum_pool(name="stp", bufs=4))
         ctx.enter_context(tc.manual_schedule())
@@ -61,10 +60,10 @@ def tile_linearmoloralayer_pa_kernel(tc, x, gate_logits, W_base, b_base, A, B, o
             r = rawp.tile([P, 4096], BF16, tag="raw")
             raws[("xa", t)] = r
 
-        def load_w(s):
+        def load_w(c, h):
             r = rawp.tile([P, 4096], BF16, tag="raw")
-            nc.sync.dma_start(out=r[:], in_=W_base[s * 256:(s + 1) * 256, :].rearrange("(p j) k -> p (j k)", j=2))
-            raws[("w", s)] = r
+            nc.sync.dma_start(out=r[:], in_=W_base[c * 512:(c + 1) * 512, :].rearrange("(p h j) k -> h p (j k)", h=2, j=2)[h])
+            raws[("w", c, h)] = r
 
         def load_b(h):
             r = rawp.tile([P, 4096], BF16, tag="raw")
@@ -93,13 +92,13 @@ def tile_linearmoloralayer_pa_kernel(tc, x, gate_logits, W_base, b_base, A, B, o
             load_x(t)
         for t in range(TT):
             load_a(t)
-        load_w(0)
-        load_w(1)
-        load_w(2)
-        load_b(0)
+        load_w(0, 0)
+        load_w(0, 1)
+        load_w(1, 0)
+        load_w(1, 1)
 
-        xc = const.tile([P, TT, 512], U32, align_bytes=64)
-        xs = const.tile([P, TT, 512], U8, align_bytes=64)
+        xc = const.tile([P, NG, 512], U32, align_bytes=64)
+        xs = const.tile([P, NG, 512], U8, align_bytes=64)
         ac = const.tile([P, 4, 512], U32, align_bytes=64)
         asc = const.tile([P, 4, 512], U8, align_bytes=64)
         bc = const.tile([P, O], U32, align_bytes=64)
@@ -107,12 +106,12 @@ def tile_linearmoloralayer_pa_kernel(tc, x, gate_logits, W_base, b_base, A, B, o
         hc = const.tile([P, 512], U32, align_bytes=64)
         hsc = const.tile([P, 512], U8, align_bytes=64)
         hwg = const.tile([P, 2048], BF16, align_bytes=64)
-        bg = const.tile([P, 4 * O], BF16, align_bytes=64)
+        hwt = const.tile([P, 4, 512], BF16)
         rt = const.tile([P, TT, P], F32)
         rexp = const.tile([P, TT, E, 4], F32)
         ex = const.tile([P, TT, E], F32)
-        keep = const.tile([P, 2 * NKEEP, 2, 256], F32)
-        bias_bc = const.tile([P, O], F32)
+        keep = const.tile([P, TT, 512], F32)
+        bias_bc = const.tile([P, O], BF16)
 
         def copy(eng, out_ap, in_ap):
             if eng == "v":
@@ -155,83 +154,90 @@ def tile_linearmoloralayer_pa_kernel(tc, x, gate_logits, W_base, b_base, A, B, o
                 nc.tensor.matmul(out=st[:], lhsT=identb[:, c:c + 1].to_broadcast([P, P]), rhs=brow[:], start=True, stop=True)
                 copy("vs"[c % 2], bias_bc[:, c * 512:(c + 1) * 512], st[:])
 
-        def flip_bank(views, words, eng, ndummy=0):
-            st = stp.tile([P, 512], F32, tag="st")
-            for i in range(ndummy):
-                dummy(st)
-            for s in range(4):
-                nc.tensor.transpose(st[:, s * P:(s + 1) * P], views[s], ident[:])
-            copy(eng, words.rearrange("p (j n u) -> p j n u", j=2, u=2), st[:].rearrange("p (j u n) -> p j n u", j=2, u=2))
+        def new_group(key):
+            grp = grpp.tile([P, 8192], BF16, tag="grp", align_bytes=64)
+            grps[key] = grp
 
         def xa_words(kind, t):
             base = 0 if kind == "x" else 1024
             return raws[("xa", t)][:].bitcast(F32)[:, base:base + 1024]
 
-        def d_xa(kind, t, eng="v"):
+        def d_a(t, eng="v"):
             di = dip.tile([P, 2048], F32, tag="di")
-            dis[(kind, t)] = di
-            copy(eng, di[:, 0:1024].rearrange("p (g u n) -> p g n u", g=4, u=2), xa_words(kind, t).rearrange("p (g n u) -> p g n u", g=4, u=2))
+            dis[("a", t)] = di
+            copy(eng, di[:, 0:1024].rearrange("p (g u n) -> p g n u", g=4, u=2), xa_words("a", t).rearrange("p (g n u) -> p g n u", g=4, u=2))
 
-        def t_xa(kind, t, nd=(0, 0), engs="ss"):
-            grp = grpp.tile([P, 2048], BF16, tag="grp", align_bytes=64)
-            grps[(kind, t)] = grp
-            words = grp[:].bitcast(F32)
+        def t_xa(kind, t, ndummy=0, engs="ss"):
+            if kind == "x":
+                dst = grps["x"][:].bitcast(F32).rearrange("p (g t n u) -> p t g n u", g=4, t=4, u=2)[:, t]
+            else:
+                dst = grps["a"][:].bitcast(F32).rearrange("p (t g n u) -> p t g n u", g=4, t=4, u=2)[:, t]
             for b in range(2):
-                if (kind, t) in dis:
-                    di = dis[(kind, t)]
-                    views = [di[:, (4 * b + s) * P:(4 * b + s + 1) * P] for s in range(4)]
-                else:
-                    w = xa_words(kind, t)
-                    views = [w[:, 256 * (2 * b + s // 2) + s % 2:256 * (2 * b + s // 2 + 1):2] for s in range(4)]
-                flip_bank(views, words[:, 512 * b:512 * (b + 1)], engs[b], nd[b])
+                st = stp.tile([P, 512], F32, tag="st")
+                if b == 0:
+                    for i in range(ndummy):
+                        dummy(st)
+                for i in range(4):
+                    if (kind, t) in dis:
+                        view = dis[(kind, t)][:, (4 * b + i) * P:(4 * b + i + 1) * P]
+                    else:
+                        w = xa_words(kind, t)
+                        view = w[:, 256 * (2 * b + i // 2) + i % 2:256 * (2 * b + i // 2 + 1):2]
+                    nc.tensor.transpose(st[:, i * P:(i + 1) * P], view, ident[:])
+                copy(engs[b], dst[:, 2 * b:2 * b + 2], st[:].rearrange("p (g u n) -> p g n u", g=2, u=2))
 
-        def q_xa(kind, t):
-            codes, scales = (xc, xs) if kind == "x" else (ac, asc)
-            nc.vector.quantize_mx(out=codes[:, t, :].bitcast(FP8X4), scales=scales[:, t, :], in_=grps[(kind, t)][:])
+        def q_x(pair):
+            for g in range(NG):
+                cols = slice(pair * 256, (pair + 1) * 256)
+                nc.vector.quantize_mx(
+                    out=xc[:, g, cols].bitcast(FP8X4),
+                    scales=xs[:, g, cols],
+                    in_=grps["x"][:, g * 2048 + pair * 1024:g * 2048 + (pair + 1) * 1024],
+                )
 
-        def d_w(s, engs="vv"):
+        def q_a(t):
+            nc.vector.quantize_mx(out=ac[:, t, :].bitcast(FP8X4), scales=asc[:, t, :], in_=grps["a"][:, t * 2048:(t + 1) * 2048])
+
+        def d_w(c, h, engs="vv"):
             di = dip.tile([P, 2048], F32, tag="di")
-            dis[("w", s)] = di
-            src = raws[("w", s)][:].bitcast(F32).rearrange("p (j g n u) -> p g j n u", j=2, g=4, u=2)
+            dis[("w", c, h)] = di
+            src = raws[("w", c, h)][:].bitcast(F32).rearrange("p (j g n u) -> p g j n u", j=2, g=4, u=2)
             dst = di[:].rearrange("p (g j u n) -> p g j n u", g=4, j=2, u=2)
-            for h in range(2):
-                copy(engs[h], dst[:, 2 * h:2 * h + 2], src[:, 2 * h:2 * h + 2])
+            for k in range(2):
+                copy(engs[k], dst[:, 2 * k:2 * k + 2], src[:, 2 * k:2 * k + 2])
 
-        def t_w(s, engs="ssss"):
-            grp = grpp.tile([P, 4096], BF16, tag="grp", align_bytes=64)
-            grps[("w", s)] = grp
-            words = grp[:].bitcast(F32)
+        def t_w(c, h, engs="ssss"):
+            if h == 0:
+                new_group(c)
+            dst = grps[c][:].bitcast(F32).rearrange("p (g n j u) -> p g n j u", g=4, j=4, u=2)
             for g in range(NG):
                 st = stp.tile([P, 512], F32, tag="st")
-                for j in range(2):
-                    for u in range(2):
-                        i = 2 * j + u
-                        if ("w", s) in dis:
-                            view = dis[("w", s)][:, (4 * g + i) * P:(4 * g + i + 1) * P]
-                        else:
-                            view = raws[("w", s)][:].bitcast(F32)[:, j * 1024 + g * 256 + u:j * 1024 + (g + 1) * 256:2]
-                        nc.tensor.transpose(st[:, i * P:(i + 1) * P], view, ident[:])
-                copy(engs[g], words[:, 512 * g:512 * (g + 1)].rearrange("p (n j u) -> p n j u", j=2, u=2), st[:].rearrange("p (j u n) -> p n j u", j=2, u=2))
+                for i in range(4):
+                    if ("w", c, h) in dis:
+                        view = dis[("w", c, h)][:, (4 * g + i) * P:(4 * g + i + 1) * P]
+                    else:
+                        j, u = i // 2, i % 2
+                        view = raws[("w", c, h)][:].bitcast(F32)[:, j * 1024 + g * 256 + u:j * 1024 + (g + 1) * 256:2]
+                    nc.tensor.transpose(st[:, i * P:(i + 1) * P], view, ident[:])
+                copy(engs[g], dst[:, g, :, 2 * h:2 * h + 2, :], st[:].rearrange("p (j u n) -> p n j u", j=2, u=2))
 
-        def q_w(s, ks=(0, 1)):
-            if ks[0] == 0:
-                wc = wcp.tile([P, 1024], U32, tag="wc", align_bytes=64)
-                ws = wcp.tile([P, 1024], U8, tag="ws", align_bytes=64)
-                wcs[s] = (wc, ws)
-            wc, ws = wcs[s]
-            for k in ks:
+        def q_w(c, gs):
+            if 0 in gs:
+                wc = wcp.tile([P, 2048], U32, tag="wc", align_bytes=64)
+                ws = wcp.tile([P, 2048], U8, tag="ws", align_bytes=64)
+                wcs[c] = (wc, ws)
+            wc, ws = wcs[c]
+            for g in gs:
                 nc.vector.quantize_mx(
-                    out=wc[:, k * 512:(k + 1) * 512].bitcast(FP8X4),
-                    scales=ws[:, k * 512:(k + 1) * 512],
-                    in_=grps[("w", s)][:, k * 2048:(k + 1) * 2048],
+                    out=wc[:, g * 512:(g + 1) * 512].bitcast(FP8X4),
+                    scales=ws[:, g * 512:(g + 1) * 512],
+                    in_=grps[c][:, g * 2048:(g + 1) * 2048],
                 )
 
         def new_acc(key):
-            tiles = []
-            for tt in range(TT):
-                a = accp.tile([P, 512], F32, tag="acc", name="acc")
-                tiles.append(a)
-            accs[key] = tiles
+            bank = accp.tile([P, 512], F32, tag="acc", name="acc")
+            accs[key] = bank
+            return bank
 
         def route_job():
             rw = rexp[:].rearrange("p t e i -> p t (e i)")
@@ -240,24 +246,28 @@ def tile_linearmoloralayer_pa_kernel(tc, x, gate_logits, W_base, b_base, A, B, o
                 nc.tensor.transpose(st[:, t * P:(t + 1) * P], rw[:, t, :], ident[:])
             nc.scalar.copy(out=rt[:].rearrange("p t n -> p (t n)"), in_=st[:])
 
-        def h_group(t, tt):
+        def h_row(t):
+            bank = new_acc(("h", t))
             for g in range(NG):
                 nc.tensor.matmul_mx(
-                    out=accs["h"][tt][:, t * P:(t + 1) * P],
+                    out=bank[:],
                     lhsT=ac[:, t, g * P:(g + 1) * P].bitcast(FP8X4),
                     lhsT_scale=asc[:, t, g * P:(g + 1) * P],
-                    rhs=xc[:, tt, g * P:(g + 1) * P].bitcast(FP8X4),
-                    rhs_scale=xs[:, tt, g * P:(g + 1) * P],
+                    rhs=xc[:, g, :].bitcast(FP8X4),
+                    rhs_scale=xs[:, g, :],
                     start=(g == 0),
                     stop=(g == NG - 1),
                 )
 
-        def hw_mult(tt):
-            nc.vector.tensor_tensor(
-                out=hwg[:, tt * 512:(tt + 1) * 512].rearrange("p (n t) -> p n t", t=4),
-                in0=accs["h"][tt][:].rearrange("p (t n) -> p n t", t=4),
-                in1=rt[:, tt, :].unsqueeze(2).to_broadcast([P, P, 4]),
-                op=ALU.mult,
+        def hw_mult(t):
+            nc.vector.tensor_tensor(out=hwt[:, t, :], in0=accs[("h", t)][:], in1=rt[:].rearrange("p t n -> p (t n)"), op=ALU.mult)
+
+        def hw_mix(half, eng):
+            n0 = half * 256
+            copy(
+                eng,
+                hwg[:, half * 1024:(half + 1) * 1024].rearrange("p (n t) -> p n t", t=4),
+                hwt[:, :, n0:n0 + 256].rearrange("p t n -> p n t"),
             )
 
         def hw_quant():
@@ -273,7 +283,9 @@ def tile_linearmoloralayer_pa_kernel(tc, x, gate_logits, W_base, b_base, A, B, o
                 copy(engs[half], dst[:, :, 16 * h:16 * h + 16], src[:, 8 * half:8 * half + 8])
 
         def t_b(half, engs):
-            bgw = bg[:].bitcast(F32).rearrange("p (n s u) -> p n s u", s=16, u=2)
+            if half == 0:
+                new_group("b")
+            bgw = grps["b"][:].bitcast(F32).rearrange("p (n s u) -> p n s u", s=16, u=2)
             for b in range(4):
                 st = stp.tile([P, 512], F32, tag="st")
                 s0 = 8 * half + 2 * b
@@ -286,196 +298,164 @@ def tile_linearmoloralayer_pa_kernel(tc, x, gate_logits, W_base, b_base, A, B, o
             nc.vector.quantize_mx(
                 out=bc[:, c * 512:(c + 1) * 512].bitcast(FP8X4),
                 scales=bsc[:, c * 512:(c + 1) * 512],
-                in_=bg[:, c * 2048:(c + 1) * 2048],
+                in_=grps["b"][:, c * 2048:(c + 1) * 2048],
             )
 
-        def half_bank(bank, tt):
-            return bank[:, (tt % 2) * 256:(tt % 2 + 1) * 256]
+        def lora(c, tts, late=False):
+            for tt in tts:
+                bank = new_acc((c, tt)) if late else accs[(c, tt)]
+                nc.tensor.matmul_mx(
+                    out=bank[:],
+                    lhsT=hc[:, tt * P:(tt + 1) * P].bitcast(FP8X4),
+                    lhsT_scale=hsc[:, tt * P:(tt + 1) * P],
+                    rhs=bc[:, c * 512:(c + 1) * 512].bitcast(FP8X4),
+                    rhs_scale=bsc[:, c * 512:(c + 1) * 512],
+                    start=late,
+                    stop=True,
+                )
 
-        def lora_pass(bank, s, tt, start):
-            nc.tensor.matmul_mx(
-                out=half_bank(bank, tt),
-                lhsT=hc[:, tt * P:(tt + 1) * P].bitcast(FP8X4),
-                lhsT_scale=hsc[:, tt * P:(tt + 1) * P],
-                rhs=bc[:, s * 256:(s + 1) * 256].bitcast(FP8X4),
-                rhs_scale=bsc[:, s * 256:(s + 1) * 256],
-                start=start,
-                stop=True,
-            )
-
-        def p_slab(s, b, lora=True, each=None):
-            bank = accp.tile([P, 512], F32, tag="acc", name="acc")
-            accs[(s, b)] = bank
-            wc, ws = wcs[s]
-            for tt in (2 * b, 2 * b + 1):
+        def base(c, tts, stop=False):
+            wc, ws = wcs[c]
+            for tt in tts:
+                bank = new_acc((c, tt))
                 for g in range(NG):
                     nc.tensor.matmul_mx(
-                        out=half_bank(bank, tt),
-                        lhsT=xc[:, tt, g * P:(g + 1) * P].bitcast(FP8X4),
-                        lhsT_scale=xs[:, tt, g * P:(g + 1) * P],
-                        rhs=wc[:, g * 256:(g + 1) * 256].bitcast(FP8X4),
-                        rhs_scale=ws[:, g * 256:(g + 1) * 256],
+                        out=bank[:],
+                        lhsT=xc[:, g, tt * P:(tt + 1) * P].bitcast(FP8X4),
+                        lhsT_scale=xs[:, g, tt * P:(tt + 1) * P],
+                        rhs=wc[:, g * 512:(g + 1) * 512].bitcast(FP8X4),
+                        rhs_scale=ws[:, g * 512:(g + 1) * 512],
                         start=(g == 0),
-                        stop=(g == NG - 1 and not lora),
+                        stop=(stop and g == NG - 1),
                     )
-                if lora:
-                    lora_pass(bank, s, tt, False)
-                if each:
-                    each(s, tt)
 
-        def pair(bank):
-            return bank[:].rearrange("p (t n) -> p t n", t=2)
+        def both(c, tts):
+            for tt in tts:
+                base(c, (tt,))
+                lora(c, (tt,))
 
-        def store(s, b, osb):
-            nc.sync.dma_start(
-                out=of[2 * b * P:(2 * b + 2) * P, s * 256:(s + 1) * 256].rearrange("(t p) n -> p t n", p=P),
-                in_=osb[:],
-            )
+        def store(c, tt, osb):
+            nc.sync.dma_start(out=of[tt * P:(tt + 1) * P, c * 512:(c + 1) * 512], in_=osb[:])
 
-        def evac(s, b):
-            bias = bias_bc[:, s * 256:(s + 1) * 256].unsqueeze(1).to_broadcast([P, 2, 256])
-            if s < NKEEP:
-                nc.vector.tensor_tensor(out=keep[:, 2 * s + b, :, :], in0=pair(accs[(s, b)]), in1=bias, op=ALU.add)
+        def evac(c, tt):
+            bias = bias_bc[:, c * 512:(c + 1) * 512]
+            if c == 0:
+                nc.vector.tensor_tensor(out=keep[:, tt, :], in0=accs[(c, tt)][:], in1=bias, op=ALU.add)
             else:
-                osb = outp.tile([P, 2, 256], F32, tag="osb")
-                nc.vector.tensor_tensor(out=osb[:], in0=pair(accs[(s, b)]), in1=bias, op=ALU.add)
-                store(s, b, osb)
+                osb = outp.tile([P, 512], F32, tag="osb")
+                nc.vector.tensor_tensor(out=osb[:], in0=accs[(c, tt)][:], in1=bias, op=ALU.add)
+                store(c, tt, osb)
 
-        def evac_one(s, tt):
-            osb = outp.tile([P, 256], F32, tag="osb")
-            cols = slice(s * 256, (s + 1) * 256)
-            nc.vector.tensor_tensor(out=osb[:], in0=half_bank(accs[(s, tt // 2)], tt), in1=bias_bc[:, cols], op=ALU.add)
-            nc.sync.dma_start(out=of[tt * P:(tt + 1) * P, cols], in_=osb[:])
+        def late_add(c, tt):
+            osb = outp.tile([P, 512], F32, tag="osb")
+            nc.vector.tensor_tensor(out=osb[:], in0=accs[(c, tt)][:], in1=keep[:, tt, :], op=ALU.add)
+            store(c, tt, osb)
 
-        def late_pass(s, b):
-            bank = accp.tile([P, 512], F32, tag="acc", name="acc")
-            accs[(s, b)] = bank
-            for tt in (2 * b, 2 * b + 1):
-                lora_pass(bank, s, tt, True)
+        def evac_halves(c, tt):
+            for k in range(2):
+                osb = outp.tile([P, 256], F32, tag="osb")
+                cols = slice(c * 512 + k * 256, c * 512 + (k + 1) * 256)
+                nc.vector.tensor_tensor(out=osb[:], in0=accs[(c, tt)][:, k * 256:(k + 1) * 256], in1=bias_bc[:, cols], op=ALU.add)
+                nc.sync.dma_start(out=of[tt * P:(tt + 1) * P, cols], in_=osb[:])
 
-        def late_add(s, b):
-            osb = outp.tile([P, 2, 256], F32, tag="osb")
-            nc.vector.tensor_tensor(out=osb[:], in0=pair(accs[(s, b)]), in1=keep[:, 2 * s + b, :, :], op=ALU.add)
-            store(s, b, osb)
-
-        def h_row(t, last=False):
-            for tt in range(TT):
-                h_group(t, tt)
-                if last:
-                    hw_mult(tt)
-        new_acc("h")
         warm_up(WARM)
         bias_job()
         softmax_head()
         softmax_tail()
-        t_xa("x", 0, (1, 0), "ss")
-        t_xa("x", 1, (1, 0), "ss")
-        q_xa("x", 0)
-        t_xa("x", 2, (1, 0), "ss")
-        q_xa("x", 1)
-        t_xa("x", 3, (1, 0), "ss")
-        q_xa("x", 2)
-        t_xa("a", 0, (1, 0))
-        q_xa("x", 3)
+        new_group("x")
+        new_group("a")
+        t_xa("x", 0, 1)
+        t_xa("x", 1, 1)
+        q_x(0)
+        t_xa("x", 2, 1)
+        t_xa("x", 3, 1)
+        t_xa("a", 0, 1)
+        q_x(1)
+        d_a(2)
         t_xa("a", 1)
-        d_xa("a", 2)
-        q_xa("a", 0)
-        t_xa("a", 2, (0, 0), "ss")
-        d_xa("a", 3)
-        q_xa("a", 1)
-        h_row(0)
+        q_a(0)
+        d_a(3)
+        t_xa("a", 2)
+        q_a(1)
         route_job()
-        t_xa("a", 3, (0, 0), "ss")
-        d_w(0)
-        load_w(3)
+        load_b(0)
         load_b(1)
-        load_w(4)
-        load_w(5)
-        q_xa("a", 2)
+        load_w(2, 0)
+        load_w(2, 1)
+        h_row(0)
+        t_xa("a", 3)
+        d_w(0, 0)
+        hw_mult(0)
+        q_a(2)
         h_row(1)
-        t_w(0)
-        d_w(1)
-        q_xa("a", 3)
+        t_w(0, 0)
+        d_w(0, 1)
+        q_a(3)
+        hw_mult(1)
         h_row(2)
-        q_w(0)
-        h_row(3, True)
-        d_w(2, "vs")
-        t_w(1)
-        p_slab(0, 0, False)
-        q_w(1, (0,))
+        t_w(0, 1)
+        d_w(1, 0)
+        h_row(3)
+        hw_mult(2)
+        q_w(0, (0, 1, 2, 3))
+        hw_mult(3)
+        t_w(1, 0)
+        d_w(1, 1, "vv")
+        base(0, (0, 1), True)
         evac(0, 0)
-        q_w(1, (1,))
-        p_slab(0, 1, False)
         evac(0, 1)
-        load_w(6)
-        t_w(2)
-        p_slab(1, 0, False)
+        load_w(3, 0)
         s_b(0, "vs")
-        d_w(3, "vv")
-        q_w(2, (0,))
-        evac(1, 0)
-        q_w(2, (1,))
-        p_slab(1, 1, False)
-        evac(1, 1)
-        load_w(7)
+        t_w(1, 1)
+        base(0, (2, 3), True)
+        q_w(1, (0, 1))
+        evac(0, 2)
+        q_w(1, (2, 3))
+        evac(0, 3)
         s_b(1, "vs")
-        t_w(3)
+        hw_mix(0, "s")
+        hw_mix(1, "v")
+        load_w(3, 1)
+        base(1, (0, 1))
+        t_b(0, "svsv")
         hw_quant()
-        p_slab(2, 0, False)
-        evac(2, 0)
-        q_w(3)
-        t_b(0, "ssvs")
-        p_slab(2, 1, False)
-        evac(2, 1)
-        d_w(4, "vv")
+        d_w(2, 0, "vs")
+        base(1, (2, 3))
         t_b(1, "svsv")
         q_b(1)
-        d_w(5, "vs")
-        t_w(4)
-        p_slab(3, 0)
-        q_w(4, (0,))
-        evac(3, 0)
-        q_w(4, (1,))
-        p_slab(3, 1)
-        evac(3, 1)
-        d_w(6, "vs")
-        t_w(5)
-        q_b(2)
-        p_slab(4, 0)
-        q_w(5, (0,))
+        t_w(2, 0)
+        d_w(2, 1, "vs")
+        lora(1, (0, 1, 2, 3))
+        evac(1, 0)
+        evac(1, 1)
+        evac(1, 2)
+        evac(1, 3)
         q_b(0)
-        evac(4, 0)
-        q_w(5, (1,))
-        p_slab(4, 1)
-        evac(4, 1)
-        late_pass(0, 0)
+        d_w(3, 0, "vs")
+        t_w(2, 1)
+        q_w(2, (0, 1))
+        lora(0, (0, 1, 2, 3), True)
         late_add(0, 0)
-        late_pass(0, 1)
+        q_b(2)
+        q_w(2, (2, 3))
         late_add(0, 1)
-        d_w(7, "vs")
-        t_w(6)
-        p_slab(5, 0)
-        q_w(6, (0,))
-        evac(5, 0)
-        q_w(6, (1,))
-        p_slab(5, 1)
-        evac(5, 1)
+        t_w(3, 0)
+        d_w(3, 1, "vs")
+        late_add(0, 2)
+        late_add(0, 3)
+        both(2, (0, 1))
+        evac(2, 0)
+        evac(2, 1)
+        t_w(3, 1)
         q_b(3)
-        late_pass(1, 0)
-        late_add(1, 0)
-        late_pass(1, 1)
-        late_add(1, 1)
-        t_w(7)
-        p_slab(6, 0)
-        q_w(7, (0,))
-        evac(6, 0)
-        q_w(7, (1,))
-        p_slab(6, 1)
-        evac(6, 1)
-        late_pass(2, 0)
-        late_add(2, 0)
-        late_pass(2, 1)
-        late_add(2, 1)
-        p_slab(7, 0)
-        evac(7, 0)
-        p_slab(7, 1, True, evac_one)
+        both(2, (2, 3))
+        q_w(3, (0, 1))
+        evac(2, 2)
+        q_w(3, (2, 3))
+        evac(2, 3)
+        both(3, (0, 1))
+        evac(3, 0)
+        evac(3, 1)
+        both(3, (2, 3))
+        evac(3, 2)
+        evac_halves(3, 3)

@@ -53,8 +53,10 @@ def tile_linearmoloralayer_pa_kernel(tc, x, gate_logits, W_base, b_base, A, B, o
         def load_a(t):
             nc.sync.dma_start(out=raws[("xa", t)][:, D:2 * D], in_=af[t, :, :])
 
-        def load_x(t):
-            nc.sync.dma_start(out=raws[("xa", t)][:, 0:D], in_=xf[t * P:(t + 1) * P, :])
+        def load_x(t, parts=1):
+            w = D // parts
+            for i in range(parts):
+                nc.sync.dma_start(out=raws[("xa", t)][:, i * w:(i + 1) * w], in_=xf[t * P:(t + 1) * P, i * w:(i + 1) * w])
 
         def raw_xa(t):
             r = rawp.tile([P, 4096], BF16, tag="raw")
@@ -70,10 +72,27 @@ def tile_linearmoloralayer_pa_kernel(tc, x, gate_logits, W_base, b_base, A, B, o
             nc.sync.dma_start(out=r[:].rearrange("p (e k) -> p e k", e=16), in_=bview[:, 16 * h:16 * h + 16, :])
             raws[("b", h)] = r
 
-        ident = const.tile([P, P], F32)
-        make_identity(nc, ident[:])
+        for t in range(TT):
+            raw_xa(t)
         brow = const.tile([P, 512], BF16)
         nc.vector.memset(brow[:].bitcast(I32), 0)
+        gl = const.tile([P, TT, E], BF16)
+        nc.sync.dma_start(out=gl[:], in_=gf.rearrange("(t p) e -> p t e", p=P))
+        nc.sync.dma_start(out=brow[0:NC, :], in_=b_base.rearrange("(c n) -> c n", c=NC))
+        load_x(0, 2)
+        load_x(1)
+        load_x(2)
+        load_x(3)
+        load_a(0)
+        load_a(1)
+        load_a(2)
+        load_a(3)
+        load_w(0, 0)
+        load_w(0, 1)
+        load_w(1, 0)
+        load_w(1, 1)
+        ident = const.tile([P, P], F32)
+        make_identity(nc, ident[:])
         zeros = const.tile([P, 512], BF16)
         nc.vector.memset(zeros[:].bitcast(I32), 0)
         ones = const.tile([P, P], BF16)
@@ -81,21 +100,8 @@ def tile_linearmoloralayer_pa_kernel(tc, x, gate_logits, W_base, b_base, A, B, o
         warm = const.tile([P, 1], F32)
         nc.vector.memset(warm[:], 0.0)
         nc.scalar.activation(out=warm[:], in_=warm[:], func=ACT.Exp)
-
         identb = const.tile([P, P], BF16)
         nc.vector.tensor_copy(out=identb[:], in_=ident[:])
-        nc.sync.dma_start(out=brow[0:NC, :], in_=b_base.rearrange("(c n) -> c n", c=NC))
-        gl = const.tile([P, TT, E], BF16)
-        nc.sync.dma_start(out=gl[:], in_=gf.rearrange("(t p) e -> p t e", p=P))
-        for t in range(TT):
-            raw_xa(t)
-            load_x(t)
-        for t in range(TT):
-            load_a(t)
-        load_w(0, 0)
-        load_w(0, 1)
-        load_w(1, 0)
-        load_w(1, 1)
 
         xc = const.tile([P, NG, 512], U32, align_bytes=64)
         xs = const.tile([P, NG, 512], U8, align_bytes=64)
@@ -246,15 +252,15 @@ def tile_linearmoloralayer_pa_kernel(tc, x, gate_logits, W_base, b_base, A, B, o
                 nc.tensor.transpose(st[:, t * P:(t + 1) * P], rw[:, t, :], ident[:])
             nc.scalar.copy(out=rt[:].rearrange("p t n -> p (t n)"), in_=st[:])
 
-        def h_row(t):
-            bank = new_acc(("h", t))
+        def h_row(t, n0=0, n1=512):
+            bank = new_acc(("h", t)) if n0 == 0 else accs[("h", t)]
             for g in range(NG):
                 nc.tensor.matmul_mx(
-                    out=bank[:],
+                    out=bank[:, n0:n1],
                     lhsT=ac[:, t, g * P:(g + 1) * P].bitcast(FP8X4),
                     lhsT_scale=asc[:, t, g * P:(g + 1) * P],
-                    rhs=xc[:, g, :].bitcast(FP8X4),
-                    rhs_scale=xs[:, g, :],
+                    rhs=xc[:, g, n0:n1].bitcast(FP8X4),
+                    rhs_scale=xs[:, g, n0:n1],
                     start=(g == 0),
                     stop=(g == NG - 1),
                 )
@@ -351,11 +357,37 @@ def tile_linearmoloralayer_pa_kernel(tc, x, gate_logits, W_base, b_base, A, B, o
             nc.vector.tensor_tensor(out=osb[:], in0=accs[(c, tt)][:], in1=keep[:, tt, :], op=ALU.add)
             store(c, tt, osb)
 
+        def both_halves(c, tt):
+            wc, ws = wcs[c]
+            for k in range(2):
+                bank = new_acc((c, tt, k))
+                for g in range(NG):
+                    gcols = slice(g * 512 + k * 256, g * 512 + (k + 1) * 256)
+                    nc.tensor.matmul_mx(
+                        out=bank[:, 0:256],
+                        lhsT=xc[:, g, tt * P:(tt + 1) * P].bitcast(FP8X4),
+                        lhsT_scale=xs[:, g, tt * P:(tt + 1) * P],
+                        rhs=wc[:, gcols].bitcast(FP8X4),
+                        rhs_scale=ws[:, gcols],
+                        start=(g == 0),
+                        stop=False,
+                    )
+                bcols = slice(c * 512 + k * 256, c * 512 + (k + 1) * 256)
+                nc.tensor.matmul_mx(
+                    out=bank[:, 0:256],
+                    lhsT=hc[:, tt * P:(tt + 1) * P].bitcast(FP8X4),
+                    lhsT_scale=hsc[:, tt * P:(tt + 1) * P],
+                    rhs=bc[:, bcols].bitcast(FP8X4),
+                    rhs_scale=bsc[:, bcols],
+                    start=False,
+                    stop=True,
+                )
+
         def evac_halves(c, tt):
             for k in range(2):
                 osb = outp.tile([P, 256], F32, tag="osb")
                 cols = slice(c * 512 + k * 256, c * 512 + (k + 1) * 256)
-                nc.vector.tensor_tensor(out=osb[:], in0=accs[(c, tt)][:, k * 256:(k + 1) * 256], in1=bias_bc[:, cols], op=ALU.add)
+                nc.vector.tensor_tensor(out=osb[:], in0=accs[(c, tt, k)][:, 0:256], in1=bias_bc[:, cols], op=ALU.add)
                 nc.sync.dma_start(out=of[tt * P:(tt + 1) * P, cols], in_=osb[:])
 
         warm_up(WARM)
@@ -364,15 +396,14 @@ def tile_linearmoloralayer_pa_kernel(tc, x, gate_logits, W_base, b_base, A, B, o
         softmax_tail()
         new_group("x")
         new_group("a")
-        t_xa("x", 0, 1)
-        t_xa("x", 1, 1)
+        t_xa("x", 0)
+        t_xa("x", 1)
         q_x(0)
-        t_xa("x", 2, 1)
-        t_xa("x", 3, 1)
-        t_xa("a", 0, 1)
-        q_x(1)
-        d_a(2)
+        t_xa("x", 2, 0, "sv")
+        t_xa("x", 3, 0, "sv")
+        t_xa("a", 0)
         t_xa("a", 1)
+        q_x(1)
         q_a(0)
         d_a(3)
         t_xa("a", 2)
@@ -409,43 +440,41 @@ def tile_linearmoloralayer_pa_kernel(tc, x, gate_logits, W_base, b_base, A, B, o
         t_w(1, 1)
         base(0, (2, 3), True)
         q_w(1, (0, 1))
+        s_b(1, "vs")
         evac(0, 2)
         q_w(1, (2, 3))
         evac(0, 3)
-        s_b(1, "vs")
+        load_w(3, 1)
+        d_w(2, 0, "vs")
+        base(1, (0,))
+        t_b(0, "svsv")
         hw_mix(0, "s")
         hw_mix(1, "v")
-        load_w(3, 1)
-        base(1, (0, 1))
-        t_b(0, "svsv")
+        base(1, (1, 2))
+        d_w(2, 1, "vs")
         hw_quant()
-        d_w(2, 0, "vs")
-        base(1, (2, 3))
         t_b(1, "svsv")
         q_b(1)
+        base(1, (3,))
         t_w(2, 0)
-        d_w(2, 1, "vs")
+        d_w(3, 0, "vv")
+        q_b(0)
         lora(1, (0, 1, 2, 3))
         evac(1, 0)
         evac(1, 1)
         evac(1, 2)
         evac(1, 3)
-        q_b(0)
-        d_w(3, 0, "vs")
-        t_w(2, 1)
-        q_w(2, (0, 1))
-        lora(0, (0, 1, 2, 3), True)
-        late_add(0, 0)
         q_b(2)
-        q_w(2, (2, 3))
-        late_add(0, 1)
+        t_w(2, 1)
+        q_w(2, (0, 1, 2, 3))
         t_w(3, 0)
         d_w(3, 1, "vs")
-        late_add(0, 2)
-        late_add(0, 3)
+        lora(0, (0, 1), True)
         both(2, (0, 1))
         evac(2, 0)
         evac(2, 1)
+        late_add(0, 0)
+        late_add(0, 1)
         t_w(3, 1)
         q_b(3)
         both(2, (2, 3))
@@ -453,9 +482,13 @@ def tile_linearmoloralayer_pa_kernel(tc, x, gate_logits, W_base, b_base, A, B, o
         evac(2, 2)
         q_w(3, (2, 3))
         evac(2, 3)
+        lora(0, (2, 3), True)
+        late_add(0, 2)
+        late_add(0, 3)
         both(3, (0, 1))
         evac(3, 0)
         evac(3, 1)
-        both(3, (2, 3))
+        both(3, (2,))
+        both_halves(3, 3)
         evac(3, 2)
         evac_halves(3, 3)

@@ -39,7 +39,7 @@ def tile_linearmoloralayer_pa_kernel(tc, x, gate_logits, W_base, b_base, A, B, o
         dip = ctx.enter_context(tc.tile_pool(name="dip", bufs=4))
         grpp = ctx.enter_context(tc.tile_pool(name="grpp", bufs=3))
         wcp = ctx.enter_context(tc.tile_pool(name="wcp", bufs=2))
-        outp = ctx.enter_context(tc.tile_pool(name="outp", bufs=4))
+        outp = ctx.enter_context(tc.tile_pool(name="outp", bufs=6))
         accp = ctx.enter_context(tc.psum_pool(name="accp", bufs=4))
         stp = ctx.enter_context(tc.psum_pool(name="stp", bufs=4))
         ctx.enter_context(tc.manual_schedule())
@@ -78,8 +78,8 @@ def tile_linearmoloralayer_pa_kernel(tc, x, gate_logits, W_base, b_base, A, B, o
         nc.vector.memset(brow[:].bitcast(I32), 0)
         gl = const.tile([P, TT, E], BF16)
         nc.sync.dma_start(out=gl[:], in_=gf.rearrange("(t p) e -> p t e", p=P))
-        nc.sync.dma_start(out=brow[0:NC, :], in_=b_base.rearrange("(c n) -> c n", c=NC))
         load_x(0, 2)
+        nc.sync.dma_start(out=brow[0:NC, :], in_=b_base.rearrange("(c n) -> c n", c=NC))
         load_x(1)
         load_x(2)
         load_x(3)
@@ -154,11 +154,12 @@ def tile_linearmoloralayer_pa_kernel(tc, x, gate_logits, W_base, b_base, A, B, o
             for i in range(n):
                 dummy(st)
 
-        def bias_job():
-            for c in range(NC):
-                st = stp.tile([P, 512], F32, tag="st")
-                nc.tensor.matmul(out=st[:], lhsT=identb[:, c:c + 1].to_broadcast([P, P]), rhs=brow[:], start=True, stop=True)
-                copy("vs"[c % 2], bias_bc[:, c * 512:(c + 1) * 512], st[:])
+        def bias_mm(c):
+            bank = new_acc(("bias", c))
+            nc.tensor.matmul(out=bank[:], lhsT=identb[:, c:c + 1].to_broadcast([P, P]), rhs=brow[:], start=True, stop=True)
+
+        def bias_out(c, eng="v"):
+            copy(eng, bias_bc[:, c * 512:(c + 1) * 512], accs[("bias", c)][:])
 
         def new_group(key):
             grp = grpp.tile([P, 8192], BF16, tag="grp", align_bytes=64)
@@ -391,14 +392,19 @@ def tile_linearmoloralayer_pa_kernel(tc, x, gate_logits, W_base, b_base, A, B, o
                 nc.sync.dma_start(out=of[tt * P:(tt + 1) * P, cols], in_=osb[:])
 
         warm_up(WARM)
-        bias_job()
         softmax_head()
         softmax_tail()
         new_group("x")
         new_group("a")
         t_xa("x", 0)
+        bias_mm(0)
+        bias_mm(1)
+        bias_out(0)
+        bias_out(1)
         t_xa("x", 1)
         q_x(0)
+        bias_mm(2)
+        bias_mm(3)
         t_xa("x", 2, 0, "sv")
         t_xa("x", 3, 0, "sv")
         t_xa("a", 0)
@@ -409,6 +415,8 @@ def tile_linearmoloralayer_pa_kernel(tc, x, gate_logits, W_base, b_base, A, B, o
         t_xa("a", 2)
         q_a(1)
         route_job()
+        bias_out(2)
+        bias_out(3, "s")
         load_b(0)
         load_b(1)
         load_w(2, 0)
@@ -440,9 +448,9 @@ def tile_linearmoloralayer_pa_kernel(tc, x, gate_logits, W_base, b_base, A, B, o
         t_w(1, 1)
         base(0, (2, 3), True)
         q_w(1, (0, 1))
-        s_b(1, "vs")
         evac(0, 2)
         q_w(1, (2, 3))
+        s_b(1, "vs")
         evac(0, 3)
         load_w(3, 1)
         d_w(2, 0, "vs")
@@ -467,9 +475,9 @@ def tile_linearmoloralayer_pa_kernel(tc, x, gate_logits, W_base, b_base, A, B, o
         q_b(2)
         t_w(2, 1)
         q_w(2, (0, 1, 2, 3))
+        lora(0, (0, 1), True)
         t_w(3, 0)
         d_w(3, 1, "vs")
-        lora(0, (0, 1), True)
         both(2, (0, 1))
         evac(2, 0)
         evac(2, 1)

@@ -103,14 +103,14 @@ def tile_linearmoloralayer_pa_kernel(tc, x, gate_logits, W_base, b_base, A, B, o
         identb = const.tile([P, P], BF16)
         nc.vector.tensor_copy(out=identb[:], in_=ident[:])
 
-        xc = const.tile([P, NG, 512], U32, align_bytes=64)
-        xs = const.tile([P, NG, 512], U8, align_bytes=64)
-        ac = const.tile([P, 4, 512], U32, align_bytes=64)
-        asc = const.tile([P, 4, 512], U8, align_bytes=64)
-        bc = const.tile([P, O], U32, align_bytes=64)
-        bsc = const.tile([P, O], U8, align_bytes=64)
-        hc = const.tile([P, 512], U32, align_bytes=64)
-        hsc = const.tile([P, 512], U8, align_bytes=64)
+        xc = const.tile([P, NG, 512], U32, align_bytes=256)
+        xs = const.tile([P, NG, 512], U8, align_bytes=256)
+        ac = const.tile([P, 4, 512], U32, align_bytes=256)
+        asc = const.tile([P, 4, 512], U8, align_bytes=256)
+        bc = const.tile([P, O], U32, align_bytes=256)
+        bsc = const.tile([P, O], U8, align_bytes=256)
+        hc = const.tile([P, 512], U32, align_bytes=256)
+        hsc = const.tile([P, 512], U8, align_bytes=256)
         hwg = const.tile([P, 2048], BF16, align_bytes=64)
         hwt = const.tile([P, 4, 512], BF16)
         rt = const.tile([P, TT, P], F32)
@@ -230,8 +230,8 @@ def tile_linearmoloralayer_pa_kernel(tc, x, gate_logits, W_base, b_base, A, B, o
 
         def q_w(c, gs):
             if 0 in gs:
-                wc = wcp.tile([P, 2048], U32, tag="wc", align_bytes=64)
-                ws = wcp.tile([P, 2048], U8, tag="ws", align_bytes=64)
+                wc = wcp.tile([P, 2048], U32, tag="wc", align_bytes=256)
+                ws = wcp.tile([P, 2048], U8, tag="ws", align_bytes=256)
                 wcs[c] = (wc, ws)
             wc, ws = wcs[c]
             for g in gs:
@@ -447,18 +447,17 @@ def tile_linearmoloralayer_pa_kernel(tc, x, gate_logits, W_base, b_base, A, B, o
         s_b(0, "vs")
         t_w(1, 1)
         base(0, (2, 3), True)
-        q_w(1, (0, 1))
+        q_w(1, (0, 1, 2, 3))
         evac(0, 2)
-        q_w(1, (2, 3))
         s_b(1, "vs")
         evac(0, 3)
         load_w(3, 1)
         d_w(2, 0, "vs")
-        base(1, (0,))
+        base(1, (0, 1))
         t_b(0, "svsv")
         hw_mix(0, "s")
         hw_mix(1, "v")
-        base(1, (1, 2))
+        base(1, (2,))
         d_w(2, 1, "vs")
         hw_quant()
         t_b(1, "svsv")

@@ -246,9 +246,11 @@ def tile_linearmoloralayer_pa_kernel(tc, x, gate_logits, W_base, b_base, A, B, o
             accs[key] = bank
             return bank
 
-        def route_job():
+        def route_job(ndummy=0):
             rw = rexp[:].rearrange("p t e i -> p t (e i)")
             st = stp.tile([P, 512], F32, tag="st")
+            for i in range(ndummy):
+                dummy(st)
             for t in range(TT):
                 nc.tensor.transpose(st[:, t * P:(t + 1) * P], rw[:, t, :], ident[:])
             nc.scalar.copy(out=rt[:].rearrange("p t n -> p (t n)"), in_=st[:])
@@ -403,18 +405,18 @@ def tile_linearmoloralayer_pa_kernel(tc, x, gate_logits, W_base, b_base, A, B, o
         bias_out(1)
         t_xa("x", 1)
         q_x(0)
-        bias_mm(2)
-        bias_mm(3)
         t_xa("x", 2, 0, "sv")
         t_xa("x", 3, 0, "sv")
         t_xa("a", 0)
+        bias_mm(2)
         t_xa("a", 1)
+        bias_mm(3)
         q_x(1)
         q_a(0)
         d_a(3)
         t_xa("a", 2)
         q_a(1)
-        route_job()
+        route_job(1)
         bias_out(2)
         bias_out(3, "s")
         load_b(0)

@@ -14,490 +14,472 @@ ACT = mybir.ActivationFunctionType
 AX = mybir.AxisListType
 
 P = 128
-TT = 4
+TOKENS = 512
+NT = 4
 D = 2048
 O = 2048
 E = 32
-R = 16
 NG = 4
 NC = 4
-FLOPS = 2 * 512 * D * O + 2 * 512 * D * 512 + 2 * 512 * 512 * O
-WARM = 3
+CH = 512
+SCALING = 2.0
+FLOPS = 2 * TOKENS * D * O + 2 * TOKENS * D * 512 + 2 * TOKENS * 512 * O
 
 
 def tile_linearmoloralayer_pa_kernel(tc, x, gate_logits, W_base, b_base, A, B, out):
     nc = tc.nc
-    xf = x.flatten_outer_dims()
-    gf = gate_logits.flatten_outer_dims()
-    af = A.flatten_outer_dims().rearrange("(p t) d -> t p d", t=4)
-    of = out.flatten_outer_dims()
-    bview = B.rearrange("e (p s) r -> p e (s r)", s=16)
+    x_rows = x.flatten_outer_dims()
+    gate_rows = gate_logits.flatten_outer_dims()
+    out_rows = out.flatten_outer_dims()
+    a_rows = A.flatten_outer_dims().rearrange("(p t) d -> t p d", t=4)
+    b_rows = B.rearrange("e (p s) r -> p e (s r)", s=16)
 
     with ExitStack() as ctx:
         const = ctx.enter_context(tc.tile_pool(name="const", bufs=1))
-        rawp = ctx.enter_context(tc.tile_pool(name="rawp", bufs=8))
-        dip = ctx.enter_context(tc.tile_pool(name="dip", bufs=4))
-        grpp = ctx.enter_context(tc.tile_pool(name="grpp", bufs=3))
-        wcp = ctx.enter_context(tc.tile_pool(name="wcp", bufs=2))
-        outp = ctx.enter_context(tc.tile_pool(name="outp", bufs=6))
-        accp = ctx.enter_context(tc.psum_pool(name="accp", bufs=4))
-        stp = ctx.enter_context(tc.psum_pool(name="stp", bufs=4))
+        raw_pool = ctx.enter_context(tc.tile_pool(name="raw", bufs=8))
+        split_pool = ctx.enter_context(tc.tile_pool(name="split", bufs=4))
+        grouped_pool = ctx.enter_context(tc.tile_pool(name="grouped", bufs=3))
+        code_pool = ctx.enter_context(tc.tile_pool(name="codes", bufs=2))
+        out_pool = ctx.enter_context(tc.tile_pool(name="out", bufs=6))
+        acc_pool = ctx.enter_context(tc.psum_pool(name="acc", bufs=4))
+        turn_pool = ctx.enter_context(tc.psum_pool(name="turn", bufs=4))
         ctx.enter_context(tc.manual_schedule())
 
-        raws = {}
-        dis = {}
-        grps = {}
-        wcs = {}
-        accs = {}
+        raw = {}
+        split = {}
+        grouped = {}
+        codes = {}
+        acc = {}
+
+        def load_x(t, pieces):
+            width = D // pieces
+            for i in range(pieces):
+                cols = slice(i * width, (i + 1) * width)
+                nc.sync.dma_start(out=raw["xa", t][:, cols], in_=x_rows[t * P:(t + 1) * P, cols])
 
         def load_a(t):
-            nc.sync.dma_start(out=raws[("xa", t)][:, D:2 * D], in_=af[t, :, :])
-
-        def load_x(t, parts=1):
-            w = D // parts
-            for i in range(parts):
-                nc.sync.dma_start(out=raws[("xa", t)][:, i * w:(i + 1) * w], in_=xf[t * P:(t + 1) * P, i * w:(i + 1) * w])
-
-        def raw_xa(t):
-            r = rawp.tile([P, 4096], BF16, tag="raw")
-            raws[("xa", t)] = r
+            nc.sync.dma_start(out=raw["xa", t][:, D:2 * D], in_=a_rows[t, :, :])
 
         def load_w(c, h):
-            r = rawp.tile([P, 4096], BF16, tag="raw")
-            nc.sync.dma_start(out=r[:], in_=W_base[c * 512:(c + 1) * 512, :].rearrange("(p h j) k -> h p (j k)", h=2, j=2)[h])
-            raws[("w", c, h)] = r
+            tile = raw_pool.tile([P, 2 * D], BF16, tag="raw")
+            raw["w", c, h] = tile
+            rows = W_base[c * CH:(c + 1) * CH, :].rearrange("(p h j) k -> h p (j k)", h=2, j=2)
+            nc.sync.dma_start(out=tile[:], in_=rows[h])
 
         def load_b(h):
-            r = rawp.tile([P, 4096], BF16, tag="raw")
-            nc.sync.dma_start(out=r[:].rearrange("p (e k) -> p e k", e=16), in_=bview[:, 16 * h:16 * h + 16, :])
-            raws[("b", h)] = r
+            tile = raw_pool.tile([P, 4096], BF16, tag="raw")
+            raw["b", h] = tile
+            nc.sync.dma_start(out=tile[:].rearrange("p (e k) -> p e k", e=16), in_=b_rows[:, 16 * h:16 * h + 16, :])
 
-        for t in range(TT):
-            raw_xa(t)
-        brow = const.tile([P, 512], BF16)
-        nc.vector.memset(brow[:].bitcast(I32), 0)
-        gl = const.tile([P, TT, E], BF16)
-        nc.sync.dma_start(out=gl[:], in_=gf.rearrange("(t p) e -> p t e", p=P))
-        load_x(0, 2)
-        nc.sync.dma_start(out=brow[0:NC, :], in_=b_base.rearrange("(c n) -> c n", c=NC))
-        load_x(1)
-        load_x(2)
-        load_x(3)
-        load_a(0)
-        load_a(1)
-        load_a(2)
-        load_a(3)
-        load_w(0, 0)
-        load_w(0, 1)
-        load_w(1, 0)
-        load_w(1, 1)
+        for t in range(NT):
+            xa = raw_pool.tile([P, 2 * D], BF16, tag="raw")
+            raw["xa", t] = xa
+        bias_rows = const.tile([P, CH], BF16)
+        nc.vector.memset(bias_rows[:].bitcast(I32), 0)
+        gates = const.tile([P, NT, E], BF16)
+        nc.sync.dma_start(out=gates[:], in_=gate_rows.rearrange("(t p) e -> p t e", p=P))
+        load_x(0, pieces=2)
+        nc.sync.dma_start(out=bias_rows[0:NC, :], in_=b_base.rearrange("(c n) -> c n", c=NC))
+        for t in range(1, NT):
+            load_x(t, pieces=1)
+        for t in range(NT):
+            load_a(t)
+        for c in range(2):
+            for h in range(2):
+                load_w(c, h)
+
         ident = const.tile([P, P], F32)
         make_identity(nc, ident[:])
-        zeros = const.tile([P, 512], BF16)
+        zeros = const.tile([P, CH], BF16)
         nc.vector.memset(zeros[:].bitcast(I32), 0)
-        ones = const.tile([P, P], BF16)
-        nc.vector.memset(ones[:], 1.0)
-        warm = const.tile([P, 1], F32)
-        nc.vector.memset(warm[:], 0.0)
-        nc.scalar.activation(out=warm[:], in_=warm[:], func=ACT.Exp)
-        identb = const.tile([P, P], BF16)
-        nc.vector.tensor_copy(out=identb[:], in_=ident[:])
+        table = const.tile([P, 1], F32)
+        nc.vector.memset(table[:], 0.0)
+        nc.scalar.activation(out=table[:], in_=table[:], func=ACT.Exp)
+        ident16 = const.tile([P, P], BF16)
+        nc.vector.tensor_copy(out=ident16[:], in_=ident[:])
 
-        xc = const.tile([P, NG, 512], U32, align_bytes=256)
-        xs = const.tile([P, NG, 512], U8, align_bytes=256)
-        ac = const.tile([P, 4, 512], U32, align_bytes=256)
-        asc = const.tile([P, 4, 512], U8, align_bytes=256)
-        bc = const.tile([P, O], U32, align_bytes=256)
-        bsc = const.tile([P, O], U8, align_bytes=256)
-        hc = const.tile([P, 512], U32, align_bytes=256)
-        hsc = const.tile([P, 512], U8, align_bytes=256)
-        hwg = const.tile([P, 2048], BF16, align_bytes=64)
-        hwt = const.tile([P, 4, 512], BF16)
-        rt = const.tile([P, TT, P], F32)
-        rexp = const.tile([P, TT, E, 4], F32)
-        ex = const.tile([P, TT, E], F32)
-        keep = const.tile([P, TT, 512], F32)
-        bias_bc = const.tile([P, O], BF16)
+        x_codes = const.tile([P, NG, TOKENS], U32, align_bytes=64)
+        x_scales = const.tile([P, NG, TOKENS], U8, align_bytes=64)
+        a_codes = const.tile([P, NT, NG * P], U32, align_bytes=64)
+        a_scales = const.tile([P, NT, NG * P], U8, align_bytes=64)
+        b_codes = const.tile([P, O], U32, align_bytes=64)
+        b_scales = const.tile([P, O], U8, align_bytes=64)
+        h_codes = const.tile([P, TOKENS], U32, align_bytes=64)
+        h_scales = const.tile([P, TOKENS], U8, align_bytes=64)
+        routed = const.tile([P, NT, TOKENS], BF16)
+        routed_mix = const.tile([P, 4 * TOKENS], BF16, align_bytes=64)
+        route_t = const.tile([P, TOKENS], F32)
+        route = const.tile([P, NT, E, 4], F32)
+        weights = const.tile([P, NT, E], F32)
+        chunk0 = const.tile([P, NT, CH], F32)
+        bias = const.tile([P, O], BF16)
 
-        def copy(eng, out_ap, in_ap):
-            if eng == "v":
-                nc.vector.tensor_copy(out=out_ap, in_=in_ap)
+        def copy(engine, dst, src):
+            if engine == "v":
+                nc.vector.tensor_copy(out=dst, in_=src)
             else:
-                nc.scalar.copy(out=out_ap, in_=in_ap)
+                nc.scalar.copy(out=dst, in_=src)
 
-        def softmax_head():
-            mx = const.tile([P, TT], F32)
-            nc.vector.tensor_reduce(out=mx[:], in_=gl[:], axis=AX.X, op=ALU.max)
-            dl = const.tile([P, TT, E], F32)
-            nc.vector.tensor_tensor(out=dl[:], in0=gl[:], in1=mx[:].unsqueeze(2).to_broadcast([P, TT, E]), op=ALU.subtract)
-            nc.scalar.activation(out=ex[:], in_=dl[:], func=ACT.Exp)
+        def new_acc(key):
+            bank = acc_pool.tile([P, CH], F32, tag="acc")
+            acc[key] = bank
+            return bank
 
-        def softmax_tail():
-            sm = const.tile([P, TT], F32)
-            nc.vector.tensor_reduce(out=sm[:], in_=ex[:], axis=AX.X, op=ALU.add)
-            rc = const.tile([P, TT], F32)
-            nc.vector.reciprocal(out=rc[:], in_=sm[:])
-            rc2 = const.tile([P, TT], F32)
-            nc.vector.tensor_scalar_mul(out=rc2[:], in0=rc[:], scalar1=2.0)
+        def new_grouped(key):
+            tile = grouped_pool.tile([P, 8192], BF16, tag="grouped", align_bytes=64)
+            grouped[key] = tile
+
+        def softmax():
+            top = const.tile([P, NT], F32)
+            nc.vector.tensor_reduce(out=top[:], in_=gates[:], axis=AX.X, op=ALU.max)
+            shifted = const.tile([P, NT, E], F32)
+            nc.vector.tensor_tensor(out=shifted[:], in0=gates[:], in1=top[:].unsqueeze(2).to_broadcast([P, NT, E]), op=ALU.subtract)
+            nc.scalar.activation(out=weights[:], in_=shifted[:], func=ACT.Exp)
+            total = const.tile([P, NT], F32)
+            nc.vector.tensor_reduce(out=total[:], in_=weights[:], axis=AX.X, op=ALU.add)
+            inverse = const.tile([P, NT], F32)
+            nc.vector.reciprocal(out=inverse[:], in_=total[:])
+            factor = const.tile([P, NT], F32)
+            nc.vector.tensor_scalar_mul(out=factor[:], in0=inverse[:], scalar1=SCALING)
             nc.vector.tensor_tensor(
-                out=rexp[:],
-                in0=ex[:].unsqueeze(3).to_broadcast([P, TT, E, 4]),
-                in1=rc2[:].unsqueeze(2).unsqueeze(3).to_broadcast([P, TT, E, 4]),
+                out=route[:],
+                in0=weights[:].unsqueeze(3).to_broadcast([P, NT, E, 4]),
+                in1=factor[:].unsqueeze(2).unsqueeze(3).to_broadcast([P, NT, E, 4]),
                 op=ALU.mult,
             )
 
-        def dummy(st):
-            nc.tensor.matmul(out=st[:], lhsT=ones[:], rhs=zeros[:], start=True, stop=True)
+        def idle_product(bank):
+            nc.tensor.matmul(out=bank[:], lhsT=zeros[:, 0:P], rhs=zeros[:], start=True, stop=True)
 
-        def warm_up(n):
-            st = stp.tile([P, 512], F32, tag="st")
-            for i in range(n):
-                dummy(st)
-
-        def bias_mm(c):
+        def bias_product(c):
             bank = new_acc(("bias", c))
-            nc.tensor.matmul(out=bank[:], lhsT=identb[:, c:c + 1].to_broadcast([P, P]), rhs=brow[:], start=True, stop=True)
+            nc.tensor.matmul(out=bank[:], lhsT=ident16[:, c:c + 1].to_broadcast([P, P]), rhs=bias_rows[:], start=True, stop=True)
 
-        def bias_out(c, eng="v"):
-            copy(eng, bias_bc[:, c * 512:(c + 1) * 512], accs[("bias", c)][:])
-
-        def new_group(key):
-            grp = grpp.tile([P, 8192], BF16, tag="grp", align_bytes=64)
-            grps[key] = grp
+        def bias_out(c, engine):
+            copy(engine, bias[:, c * CH:(c + 1) * CH], acc["bias", c][:])
 
         def xa_words(kind, t):
-            base = 0 if kind == "x" else 1024
-            return raws[("xa", t)][:].bitcast(F32)[:, base:base + 1024]
+            first = 0 if kind == "x" else D // 2
+            return raw["xa", t][:].bitcast(F32)[:, first:first + D // 2]
 
-        def d_a(t, eng="v"):
-            di = dip.tile([P, 2048], F32, tag="di")
-            dis[("a", t)] = di
-            copy(eng, di[:, 0:1024].rearrange("p (g u n) -> p g n u", g=4, u=2), xa_words("a", t).rearrange("p (g n u) -> p g n u", g=4, u=2))
+        def split_a(t):
+            tile = split_pool.tile([P, D], F32, tag="split")
+            split["a", t] = tile
+            src = xa_words("a", t).rearrange("p (g n u) -> p g n u", g=NG, u=2)
+            copy("v", tile[:, 0:D // 2].rearrange("p (g u n) -> p g n u", g=NG, u=2), src)
 
-        def t_xa(kind, t, ndummy=0, engs="ss"):
-            if kind == "x":
-                dst = grps["x"][:].bitcast(F32).rearrange("p (g t n u) -> p t g n u", g=4, t=4, u=2)[:, t]
-            else:
-                dst = grps["a"][:].bitcast(F32).rearrange("p (t g n u) -> p t g n u", g=4, t=4, u=2)[:, t]
+        def turn_xa(kind, t, engines):
+            order = "p (g t n u) -> p t g n u" if kind == "x" else "p (t g n u) -> p t g n u"
+            dst = grouped[kind][:].bitcast(F32).rearrange(order, g=NG, t=NT, u=2)[:, t]
             for b in range(2):
-                st = stp.tile([P, 512], F32, tag="st")
-                if b == 0:
-                    for i in range(ndummy):
-                        dummy(st)
+                bank = turn_pool.tile([P, CH], F32, tag="turn")
                 for i in range(4):
-                    if (kind, t) in dis:
-                        view = dis[(kind, t)][:, (4 * b + i) * P:(4 * b + i + 1) * P]
+                    g, u = 2 * b + i // 2, i % 2
+                    if (kind, t) in split:
+                        words = split[kind, t][:, (2 * g + u) * P:(2 * g + u + 1) * P]
                     else:
-                        w = xa_words(kind, t)
-                        view = w[:, 256 * (2 * b + i // 2) + i % 2:256 * (2 * b + i // 2 + 1):2]
-                    nc.tensor.transpose(st[:, i * P:(i + 1) * P], view, ident[:])
-                copy(engs[b], dst[:, 2 * b:2 * b + 2], st[:].rearrange("p (g u n) -> p g n u", g=2, u=2))
+                        words = xa_words(kind, t)[:, 256 * g + u:256 * (g + 1):2]
+                    nc.tensor.transpose(bank[:, i * P:(i + 1) * P], words, ident[:])
+                copy(engines[b], dst[:, 2 * b:2 * b + 2], bank[:].rearrange("p (g u n) -> p g n u", g=2, u=2))
 
-        def q_x(pair):
+        def quantize_x(pair):
+            tokens = slice(pair * 2 * P, (pair + 1) * 2 * P)
             for g in range(NG):
-                cols = slice(pair * 256, (pair + 1) * 256)
+                first = g * 2048 + pair * 1024
                 nc.vector.quantize_mx(
-                    out=xc[:, g, cols].bitcast(FP8X4),
-                    scales=xs[:, g, cols],
-                    in_=grps["x"][:, g * 2048 + pair * 1024:g * 2048 + (pair + 1) * 1024],
+                    out=x_codes[:, g, tokens].bitcast(FP8X4),
+                    scales=x_scales[:, g, tokens],
+                    in_=grouped["x"][:, first:first + 1024],
                 )
 
-        def q_a(t):
-            nc.vector.quantize_mx(out=ac[:, t, :].bitcast(FP8X4), scales=asc[:, t, :], in_=grps["a"][:, t * 2048:(t + 1) * 2048])
+        def quantize_a(t):
+            nc.vector.quantize_mx(
+                out=a_codes[:, t, :].bitcast(FP8X4),
+                scales=a_scales[:, t, :],
+                in_=grouped["a"][:, t * 2048:(t + 1) * 2048],
+            )
 
-        def d_w(c, h, engs="vv"):
-            di = dip.tile([P, 2048], F32, tag="di")
-            dis[("w", c, h)] = di
-            src = raws[("w", c, h)][:].bitcast(F32).rearrange("p (j g n u) -> p g j n u", j=2, g=4, u=2)
-            dst = di[:].rearrange("p (g j u n) -> p g j n u", g=4, j=2, u=2)
+        def split_w(c, h, engines):
+            tile = split_pool.tile([P, D], F32, tag="split")
+            split["w", c, h] = tile
+            src = raw["w", c, h][:].bitcast(F32).rearrange("p (j g n u) -> p g j n u", j=2, g=NG, u=2)
+            dst = tile[:].rearrange("p (g j u n) -> p g j n u", g=NG, j=2, u=2)
             for k in range(2):
-                copy(engs[k], dst[:, 2 * k:2 * k + 2], src[:, 2 * k:2 * k + 2])
+                copy(engines[k], dst[:, 2 * k:2 * k + 2], src[:, 2 * k:2 * k + 2])
 
-        def t_w(c, h, engs="ssss"):
+        def turn_w(c, h):
             if h == 0:
-                new_group(c)
-            dst = grps[c][:].bitcast(F32).rearrange("p (g n j u) -> p g n j u", g=4, j=4, u=2)
+                new_grouped(("w", c))
+            dst = grouped["w", c][:].bitcast(F32).rearrange("p (g n j u) -> p g n j u", g=NG, j=4, u=2)
             for g in range(NG):
-                st = stp.tile([P, 512], F32, tag="st")
+                bank = turn_pool.tile([P, CH], F32, tag="turn")
                 for i in range(4):
-                    if ("w", c, h) in dis:
-                        view = dis[("w", c, h)][:, (4 * g + i) * P:(4 * g + i + 1) * P]
-                    else:
-                        j, u = i // 2, i % 2
-                        view = raws[("w", c, h)][:].bitcast(F32)[:, j * 1024 + g * 256 + u:j * 1024 + (g + 1) * 256:2]
-                    nc.tensor.transpose(st[:, i * P:(i + 1) * P], view, ident[:])
-                copy(engs[g], dst[:, g, :, 2 * h:2 * h + 2, :], st[:].rearrange("p (j u n) -> p n j u", j=2, u=2))
+                    words = split["w", c, h][:, (4 * g + i) * P:(4 * g + i + 1) * P]
+                    nc.tensor.transpose(bank[:, i * P:(i + 1) * P], words, ident[:])
+                copy("s", dst[:, g, :, 2 * h:2 * h + 2, :], bank[:].rearrange("p (j u n) -> p n j u", j=2, u=2))
 
-        def q_w(c, gs):
-            if 0 in gs:
-                wc = wcp.tile([P, 2048], U32, tag="wc", align_bytes=256)
-                ws = wcp.tile([P, 2048], U8, tag="ws", align_bytes=256)
-                wcs[c] = (wc, ws)
-            wc, ws = wcs[c]
-            for g in gs:
+        def quantize_w(c, passes):
+            if 0 in passes:
+                w_codes = code_pool.tile([P, NG * CH], U32, tag="codes", align_bytes=64)
+                w_scales = code_pool.tile([P, NG * CH], U8, tag="scales", align_bytes=64)
+                codes[c] = (w_codes, w_scales)
+            w_codes, w_scales = codes[c]
+            for g in passes:
                 nc.vector.quantize_mx(
-                    out=wc[:, g * 512:(g + 1) * 512].bitcast(FP8X4),
-                    scales=ws[:, g * 512:(g + 1) * 512],
-                    in_=grps[c][:, g * 2048:(g + 1) * 2048],
+                    out=w_codes[:, g * CH:(g + 1) * CH].bitcast(FP8X4),
+                    scales=w_scales[:, g * CH:(g + 1) * CH],
+                    in_=grouped["w", c][:, g * 2048:(g + 1) * 2048],
                 )
 
-        def new_acc(key):
-            bank = accp.tile([P, 512], F32, tag="acc", name="acc")
-            accs[key] = bank
-            return bank
+        def split_b(h, engines):
+            src = raw["b", h][:].bitcast(F32).rearrange("p (e s v u) -> p s e v u", e=16, s=16, v=4)
+            for k in range(2):
+                if h == 0:
+                    tile = split_pool.tile([P, D], F32, tag="split")
+                    split["b", k] = tile
+                dst = split["b", k][:].rearrange("p (s u e v) -> p s e v u", s=8, u=2, v=4)
+                copy(engines[k], dst[:, :, 16 * h:16 * h + 16], src[:, 8 * k:8 * k + 8])
 
-        def route_job(ndummy=0):
-            rw = rexp[:].rearrange("p t e i -> p t (e i)")
-            st = stp.tile([P, 512], F32, tag="st")
-            for i in range(ndummy):
-                dummy(st)
-            for t in range(TT):
-                nc.tensor.transpose(st[:, t * P:(t + 1) * P], rw[:, t, :], ident[:])
-            nc.scalar.copy(out=rt[:].rearrange("p t n -> p (t n)"), in_=st[:])
+        def turn_b(k):
+            if k == 0:
+                new_grouped("b")
+            dst = grouped["b"][:].bitcast(F32).rearrange("p (n s u) -> p n s u", s=16, u=2)
+            for b in range(4):
+                bank = turn_pool.tile([P, CH], F32, tag="turn")
+                for i in range(4):
+                    words = split["b", k][:, (4 * b + i) * P:(4 * b + i + 1) * P]
+                    nc.tensor.transpose(bank[:, i * P:(i + 1) * P], words, ident[:])
+                s = 8 * k + 2 * b
+                copy("sv"[b % 2], dst[:, :, s:s + 2, :], bank[:].rearrange("p (s u n) -> p n s u", s=2, u=2))
 
-        def h_row(t, n0=0, n1=512):
-            bank = new_acc(("h", t)) if n0 == 0 else accs[("h", t)]
+        def quantize_b(c):
+            nc.vector.quantize_mx(
+                out=b_codes[:, c * CH:(c + 1) * CH].bitcast(FP8X4),
+                scales=b_scales[:, c * CH:(c + 1) * CH],
+                in_=grouped["b"][:, c * 2048:(c + 1) * 2048],
+            )
+
+        def h_product(t):
+            bank = new_acc(("h", t))
             for g in range(NG):
                 nc.tensor.matmul_mx(
-                    out=bank[:, n0:n1],
-                    lhsT=ac[:, t, g * P:(g + 1) * P].bitcast(FP8X4),
-                    lhsT_scale=asc[:, t, g * P:(g + 1) * P],
-                    rhs=xc[:, g, n0:n1].bitcast(FP8X4),
-                    rhs_scale=xs[:, g, n0:n1],
+                    out=bank[:],
+                    lhsT=a_codes[:, t, g * P:(g + 1) * P].bitcast(FP8X4),
+                    lhsT_scale=a_scales[:, t, g * P:(g + 1) * P],
+                    rhs=x_codes[:, g, :].bitcast(FP8X4),
+                    rhs_scale=x_scales[:, g, :],
                     start=(g == 0),
                     stop=(g == NG - 1),
                 )
 
-        def hw_mult(t):
-            nc.vector.tensor_tensor(out=hwt[:, t, :], in0=accs[("h", t)][:], in1=rt[:].rearrange("p t n -> p (t n)"), op=ALU.mult)
+        def turn_route():
+            bank = turn_pool.tile([P, CH], F32, tag="turn")
+            idle_product(bank)
+            rows = route[:].rearrange("p t e i -> p t (e i)")
+            for t in range(NT):
+                nc.tensor.transpose(bank[:, t * P:(t + 1) * P], rows[:, t, :], ident[:])
+            nc.scalar.copy(out=route_t[:], in_=bank[:])
 
-        def hw_mix(half, eng):
-            n0 = half * 256
+        def h_route(t):
+            nc.vector.tensor_tensor(out=routed[:, t, :], in0=acc["h", t][:], in1=route_t[:], op=ALU.mult)
+
+        def h_mix(half, engine):
+            tokens = slice(half * 256, (half + 1) * 256)
             copy(
-                eng,
-                hwg[:, half * 1024:(half + 1) * 1024].rearrange("p (n t) -> p n t", t=4),
-                hwt[:, :, n0:n0 + 256].rearrange("p t n -> p n t"),
+                engine,
+                routed_mix[:, half * 1024:(half + 1) * 1024].rearrange("p (n t) -> p n t", t=4),
+                routed[:, :, tokens].rearrange("p t n -> p n t"),
             )
 
-        def hw_quant():
-            nc.vector.quantize_mx(out=hc[:].bitcast(FP8X4), scales=hsc[:], in_=hwg[:])
+        def h_quantize():
+            nc.vector.quantize_mx(out=h_codes[:].bitcast(FP8X4), scales=h_scales[:], in_=routed_mix[:])
 
-        def s_b(h, engs="vv"):
-            src = raws[("b", h)][:].bitcast(F32).rearrange("p (e s v u) -> p s e v u", e=16, s=16, v=4)
-            for half in range(2):
-                if h == 0:
-                    di = dip.tile([P, 2048], F32, tag="di")
-                    dis[("b", half)] = di
-                dst = dis[("b", half)][:].rearrange("p (s u e v) -> p s e v u", s=8, u=2, v=4)
-                copy(engs[half], dst[:, :, 16 * h:16 * h + 16], src[:, 8 * half:8 * half + 8])
+        def base_passes(bank, c, t, first, width, last):
+            w_codes, w_scales = codes[c]
+            for g in range(NG):
+                cols = slice(g * CH + first, g * CH + first + width)
+                nc.tensor.matmul_mx(
+                    out=bank[:, 0:width],
+                    lhsT=x_codes[:, g, t * P:(t + 1) * P].bitcast(FP8X4),
+                    lhsT_scale=x_scales[:, g, t * P:(t + 1) * P],
+                    rhs=w_codes[:, cols].bitcast(FP8X4),
+                    rhs_scale=w_scales[:, cols],
+                    start=(g == 0),
+                    stop=(last and g == NG - 1),
+                )
 
-        def t_b(half, engs):
-            if half == 0:
-                new_group("b")
-            bgw = grps["b"][:].bitcast(F32).rearrange("p (n s u) -> p n s u", s=16, u=2)
-            for b in range(4):
-                st = stp.tile([P, 512], F32, tag="st")
-                s0 = 8 * half + 2 * b
-                for i in range(4):
-                    col = (2 * (2 * b + i // 2) + i % 2) * P
-                    nc.tensor.transpose(st[:, i * P:(i + 1) * P], dis[("b", half)][:, col:col + P], ident[:])
-                copy(engs[b], bgw[:, :, s0:s0 + 2, :], st[:].rearrange("p (s u n) -> p n s u", s=2, u=2))
-
-        def q_b(c):
-            nc.vector.quantize_mx(
-                out=bc[:, c * 512:(c + 1) * 512].bitcast(FP8X4),
-                scales=bsc[:, c * 512:(c + 1) * 512],
-                in_=grps["b"][:, c * 2048:(c + 1) * 2048],
+        def adapter_pass(bank, c, t, first, width, alone):
+            cols = slice(c * CH + first, c * CH + first + width)
+            nc.tensor.matmul_mx(
+                out=bank[:, 0:width],
+                lhsT=h_codes[:, t * P:(t + 1) * P].bitcast(FP8X4),
+                lhsT_scale=h_scales[:, t * P:(t + 1) * P],
+                rhs=b_codes[:, cols].bitcast(FP8X4),
+                rhs_scale=b_scales[:, cols],
+                start=alone,
+                stop=True,
             )
 
-        def lora(c, tts, late=False):
-            for tt in tts:
-                bank = new_acc((c, tt)) if late else accs[(c, tt)]
-                nc.tensor.matmul_mx(
-                    out=bank[:],
-                    lhsT=hc[:, tt * P:(tt + 1) * P].bitcast(FP8X4),
-                    lhsT_scale=hsc[:, tt * P:(tt + 1) * P],
-                    rhs=bc[:, c * 512:(c + 1) * 512].bitcast(FP8X4),
-                    rhs_scale=bsc[:, c * 512:(c + 1) * 512],
-                    start=late,
-                    stop=True,
-                )
+        def base(c, t, last=False):
+            base_passes(new_acc((c, t)), c, t, 0, CH, last)
 
-        def base(c, tts, stop=False):
-            wc, ws = wcs[c]
-            for tt in tts:
-                bank = new_acc((c, tt))
-                for g in range(NG):
-                    nc.tensor.matmul_mx(
-                        out=bank[:],
-                        lhsT=xc[:, g, tt * P:(tt + 1) * P].bitcast(FP8X4),
-                        lhsT_scale=xs[:, g, tt * P:(tt + 1) * P],
-                        rhs=wc[:, g * 512:(g + 1) * 512].bitcast(FP8X4),
-                        rhs_scale=ws[:, g * 512:(g + 1) * 512],
-                        start=(g == 0),
-                        stop=(stop and g == NG - 1),
-                    )
+        def adapter(c, t):
+            adapter_pass(acc[c, t], c, t, 0, CH, alone=False)
 
-        def both(c, tts):
-            for tt in tts:
-                base(c, (tt,))
-                lora(c, (tt,))
+        def both(c, t):
+            base(c, t)
+            adapter(c, t)
 
-        def store(c, tt, osb):
-            nc.sync.dma_start(out=of[tt * P:(tt + 1) * P, c * 512:(c + 1) * 512], in_=osb[:])
+        def store(c, t, first, width, tile):
+            cols = slice(c * CH + first, c * CH + first + width)
+            nc.sync.dma_start(out=out_rows[t * P:(t + 1) * P, cols], in_=tile[:])
 
-        def evac(c, tt):
-            bias = bias_bc[:, c * 512:(c + 1) * 512]
-            if c == 0:
-                nc.vector.tensor_tensor(out=keep[:, tt, :], in0=accs[(c, tt)][:], in1=bias, op=ALU.add)
-            else:
-                osb = outp.tile([P, 512], F32, tag="osb")
-                nc.vector.tensor_tensor(out=osb[:], in0=accs[(c, tt)][:], in1=bias, op=ALU.add)
-                store(c, tt, osb)
+        def finish(c, t):
+            tile = out_pool.tile([P, CH], F32, tag="out")
+            nc.vector.tensor_tensor(out=tile[:], in0=acc[c, t][:], in1=bias[:, c * CH:(c + 1) * CH], op=ALU.add)
+            store(c, t, 0, CH, tile)
 
-        def late_add(c, tt):
-            osb = outp.tile([P, 512], F32, tag="osb")
-            nc.vector.tensor_tensor(out=osb[:], in0=accs[(c, tt)][:], in1=keep[:, tt, :], op=ALU.add)
-            store(c, tt, osb)
+        def finish_base0(t):
+            nc.vector.tensor_tensor(out=chunk0[:, t, :], in0=acc[0, t][:], in1=bias[:, 0:CH], op=ALU.add)
 
-        def both_halves(c, tt):
-            wc, ws = wcs[c]
-            for k in range(2):
-                bank = new_acc((c, tt, k))
-                for g in range(NG):
-                    gcols = slice(g * 512 + k * 256, g * 512 + (k + 1) * 256)
-                    nc.tensor.matmul_mx(
-                        out=bank[:, 0:256],
-                        lhsT=xc[:, g, tt * P:(tt + 1) * P].bitcast(FP8X4),
-                        lhsT_scale=xs[:, g, tt * P:(tt + 1) * P],
-                        rhs=wc[:, gcols].bitcast(FP8X4),
-                        rhs_scale=ws[:, gcols],
-                        start=(g == 0),
-                        stop=False,
-                    )
-                bcols = slice(c * 512 + k * 256, c * 512 + (k + 1) * 256)
-                nc.tensor.matmul_mx(
-                    out=bank[:, 0:256],
-                    lhsT=hc[:, tt * P:(tt + 1) * P].bitcast(FP8X4),
-                    lhsT_scale=hsc[:, tt * P:(tt + 1) * P],
-                    rhs=bc[:, bcols].bitcast(FP8X4),
-                    rhs_scale=bsc[:, bcols],
-                    start=False,
-                    stop=True,
-                )
+        def adapter0(t):
+            adapter_pass(new_acc((0, t)), 0, t, 0, CH, alone=True)
 
-        def evac_halves(c, tt):
-            for k in range(2):
-                osb = outp.tile([P, 256], F32, tag="osb")
-                cols = slice(c * 512 + k * 256, c * 512 + (k + 1) * 256)
-                nc.vector.tensor_tensor(out=osb[:], in0=accs[(c, tt, k)][:, 0:256], in1=bias_bc[:, cols], op=ALU.add)
-                nc.sync.dma_start(out=of[tt * P:(tt + 1) * P, cols], in_=osb[:])
+        def finish0(t):
+            tile = out_pool.tile([P, CH], F32, tag="out")
+            nc.vector.tensor_tensor(out=tile[:], in0=acc[0, t][:], in1=chunk0[:, t, :], op=ALU.add)
+            store(0, t, 0, CH, tile)
 
-        warm_up(WARM)
-        softmax_head()
-        softmax_tail()
-        new_group("x")
-        new_group("a")
-        t_xa("x", 0)
-        bias_mm(0)
-        bias_mm(1)
-        bias_out(0)
-        bias_out(1)
-        t_xa("x", 1)
-        q_x(0)
-        t_xa("x", 2, 0, "sv")
-        t_xa("x", 3, 0, "sv")
-        t_xa("a", 0)
-        bias_mm(2)
-        t_xa("a", 1)
-        bias_mm(3)
-        q_x(1)
-        q_a(0)
-        d_a(3)
-        t_xa("a", 2)
-        q_a(1)
-        route_job(1)
-        bias_out(2)
+        HALF = CH // 2
+
+        def both_half(c, t, k):
+            bank = new_acc((c, t, k))
+            base_passes(bank, c, t, k * HALF, HALF, last=False)
+            adapter_pass(bank, c, t, k * HALF, HALF, alone=False)
+
+        def finish_half(c, t, k):
+            tile = out_pool.tile([P, HALF], F32, tag="out")
+            cols = slice(c * CH + k * HALF, c * CH + (k + 1) * HALF)
+            nc.vector.tensor_tensor(out=tile[:], in0=acc[c, t, k][:, 0:HALF], in1=bias[:, cols], op=ALU.add)
+            store(c, t, k * HALF, HALF, tile)
+
+        idle_bank = turn_pool.tile([P, CH], F32, tag="turn")
+        for i in range(3):
+            idle_product(idle_bank)
+        softmax()
+        new_grouped("x")
+        new_grouped("a")
+        turn_xa("x", 0, "ss")
+        bias_product(0)
+        bias_product(1)
+        bias_out(0, "v")
+        bias_out(1, "v")
+        turn_xa("x", 1, "ss")
+        quantize_x(0)
+        turn_xa("x", 2, "sv")
+        turn_xa("x", 3, "sv")
+        turn_xa("a", 0, "ss")
+        bias_product(2)
+        turn_xa("a", 1, "ss")
+        bias_product(3)
+        quantize_x(1)
+        quantize_a(0)
+        split_a(3)
+        turn_xa("a", 2, "ss")
+        quantize_a(1)
+        turn_route()
+        bias_out(2, "v")
         bias_out(3, "s")
         load_b(0)
         load_b(1)
         load_w(2, 0)
         load_w(2, 1)
-        h_row(0)
-        t_xa("a", 3)
-        d_w(0, 0)
-        hw_mult(0)
-        q_a(2)
-        h_row(1)
-        t_w(0, 0)
-        d_w(0, 1)
-        q_a(3)
-        hw_mult(1)
-        h_row(2)
-        t_w(0, 1)
-        d_w(1, 0)
-        h_row(3)
-        hw_mult(2)
-        q_w(0, (0, 1, 2, 3))
-        hw_mult(3)
-        t_w(1, 0)
-        d_w(1, 1, "vv")
-        base(0, (0, 1), True)
-        evac(0, 0)
-        evac(0, 1)
+        h_product(0)
+        turn_xa("a", 3, "ss")
+        split_w(0, 0, "vv")
+        h_route(0)
+        quantize_a(2)
+        h_product(1)
+        turn_w(0, 0)
+        split_w(0, 1, "vv")
+        quantize_a(3)
+        h_route(1)
+        h_product(2)
+        turn_w(0, 1)
+        split_w(1, 0, "vv")
+        h_product(3)
+        h_route(2)
+        quantize_w(0, (0, 1, 2, 3))
+        h_route(3)
+
+        turn_w(1, 0)
+        split_w(1, 1, "vv")
+        base(0, 0, last=True)
+        base(0, 1, last=True)
+        finish_base0(0)
+        finish_base0(1)
         load_w(3, 0)
-        s_b(0, "vs")
-        t_w(1, 1)
-        base(0, (2, 3), True)
-        q_w(1, (0, 1, 2, 3))
-        evac(0, 2)
-        s_b(1, "vs")
-        evac(0, 3)
+        split_b(0, "vs")
+        turn_w(1, 1)
+        base(0, 2, last=True)
+        base(0, 3, last=True)
+        quantize_w(1, (0, 1, 2, 3))
+        finish_base0(2)
+        split_b(1, "vs")
+        finish_base0(3)
         load_w(3, 1)
-        d_w(2, 0, "vs")
-        base(1, (0, 1))
-        t_b(0, "svsv")
-        hw_mix(0, "s")
-        hw_mix(1, "v")
-        base(1, (2,))
-        d_w(2, 1, "vs")
-        hw_quant()
-        t_b(1, "svsv")
-        q_b(1)
-        base(1, (3,))
-        t_w(2, 0)
-        d_w(3, 0, "vv")
-        q_b(0)
-        lora(1, (0, 1, 2, 3))
-        evac(1, 0)
-        evac(1, 1)
-        evac(1, 2)
-        evac(1, 3)
-        q_b(2)
-        t_w(2, 1)
-        q_w(2, (0, 1, 2, 3))
-        lora(0, (0, 1), True)
-        t_w(3, 0)
-        d_w(3, 1, "vs")
-        both(2, (0, 1))
-        evac(2, 0)
-        evac(2, 1)
-        late_add(0, 0)
-        late_add(0, 1)
-        t_w(3, 1)
-        q_b(3)
-        both(2, (2, 3))
-        q_w(3, (0, 1))
-        evac(2, 2)
-        q_w(3, (2, 3))
-        evac(2, 3)
-        lora(0, (2, 3), True)
-        late_add(0, 2)
-        late_add(0, 3)
-        both(3, (0, 1))
-        evac(3, 0)
-        evac(3, 1)
-        both(3, (2,))
-        both_halves(3, 3)
-        evac(3, 2)
-        evac_halves(3, 3)
+        split_w(2, 0, "vs")
+        base(1, 0)
+        base(1, 1)
+        turn_b(0)
+        h_mix(0, "s")
+        h_mix(1, "v")
+        base(1, 2)
+        split_w(2, 1, "vs")
+        h_quantize()
+        turn_b(1)
+        quantize_b(1)
+        base(1, 3)
+        turn_w(2, 0)
+        split_w(3, 0, "vv")
+        quantize_b(0)
+        for t in range(NT):
+            adapter(1, t)
+        for t in range(NT):
+            finish(1, t)
+
+        turn_w(2, 1)
+        quantize_w(2, (0, 1, 2, 3))
+        quantize_b(2)
+        adapter0(0)
+        adapter0(1)
+        turn_w(3, 0)
+        split_w(3, 1, "vs")
+        both(2, 0)
+        both(2, 1)
+        finish0(0)
+        finish(2, 0)
+        finish0(1)
+        finish(2, 1)
+        turn_w(3, 1)
+        quantize_b(3)
+        both(2, 2)
+        both(2, 3)
+        quantize_w(3, (0, 1))
+        finish(2, 2)
+        quantize_w(3, (2, 3))
+        finish(2, 3)
+        adapter0(2)
+        adapter0(3)
+        finish0(2)
+        finish0(3)
+        both(3, 0)
+        both(3, 1)
+        finish(3, 0)
+        finish(3, 1)
+        both(3, 2)
+        both_half(3, 3, 0)
+        both_half(3, 3, 1)
+        finish(3, 2)
+        finish_half(3, 3, 0)
+        finish_half(3, 3, 1)

from contextlib import ExitStack

import concourse.mybir as mybir
from concourse.masks import make_identity

F32 = mybir.dt.float32
BF16 = mybir.dt.bfloat16
U32 = mybir.dt.uint32
U8 = mybir.dt.uint8
I32 = mybir.dt.int32
FP8X4 = mybir.dt.float8_e4m3fn_x4
ALU = mybir.AluOpType
ACT = mybir.ActivationFunctionType
AX = mybir.AxisListType

P = 128
TOKENS = 512
NT = 4
D = 2048
O = 2048
E = 32
NG = 4
NC = 4
CH = 512
SCALING = 2.0
FLOPS = 2 * TOKENS * D * O + 2 * TOKENS * D * 512 + 2 * TOKENS * 512 * O


def tile_linearmoloralayer_pa_kernel(tc, x, gate_logits, W_base, b_base, A, B, out):
    nc = tc.nc
    x_rows = x.flatten_outer_dims()
    gate_rows = gate_logits.flatten_outer_dims()
    out_rows = out.flatten_outer_dims()
    a_rows = A.flatten_outer_dims().rearrange("(p t) d -> t p d", t=4)
    b_rows = B.rearrange("e (p s) r -> p e (s r)", s=16)

    with ExitStack() as ctx:
        const = ctx.enter_context(tc.tile_pool(name="const", bufs=1))
        raw_pool = ctx.enter_context(tc.tile_pool(name="raw", bufs=8))
        split_pool = ctx.enter_context(tc.tile_pool(name="split", bufs=4))
        grouped_pool = ctx.enter_context(tc.tile_pool(name="grouped", bufs=3))
        code_pool = ctx.enter_context(tc.tile_pool(name="codes", bufs=2))
        out_pool = ctx.enter_context(tc.tile_pool(name="out", bufs=6))
        acc_pool = ctx.enter_context(tc.psum_pool(name="acc", bufs=4))
        turn_pool = ctx.enter_context(tc.psum_pool(name="turn", bufs=4))
        ctx.enter_context(tc.manual_schedule())

        raw = {}
        split = {}
        grouped = {}
        codes = {}
        acc = {}

        def load_x(t, pieces):
            width = D // pieces
            for i in range(pieces):
                cols = slice(i * width, (i + 1) * width)
                nc.sync.dma_start(out=raw["xa", t][:, cols], in_=x_rows[t * P:(t + 1) * P, cols])

        def load_a(t):
            nc.sync.dma_start(out=raw["xa", t][:, D:2 * D], in_=a_rows[t, :, :])

        def load_w(c, h):
            tile = raw_pool.tile([P, 2 * D], BF16, tag="raw")
            raw["w", c, h] = tile
            rows = W_base[c * CH:(c + 1) * CH, :].rearrange("(p h j) k -> h p (j k)", h=2, j=2)
            nc.sync.dma_start(out=tile[:], in_=rows[h])

        def load_b(h):
            tile = raw_pool.tile([P, 4096], BF16, tag="raw")
            raw["b", h] = tile
            nc.sync.dma_start(out=tile[:].rearrange("p (e k) -> p e k", e=16), in_=b_rows[:, 16 * h:16 * h + 16, :])

        for t in range(NT):
            xa = raw_pool.tile([P, 2 * D], BF16, tag="raw")
            raw["xa", t] = xa
        bias_rows = const.tile([P, CH], BF16)
        nc.vector.memset(bias_rows[:].bitcast(I32), 0)
        gates = const.tile([P, NT, E], BF16)
        nc.sync.dma_start(out=gates[:], in_=gate_rows.rearrange("(t p) e -> p t e", p=P))
        load_x(0, pieces=2)
        nc.sync.dma_start(out=bias_rows[0:NC, :], in_=b_base.rearrange("(c n) -> c n", c=NC))
        for t in range(1, NT):
            load_x(t, pieces=1)
        for t in range(NT):
            load_a(t)
        for c in range(2):
            for h in range(2):
                load_w(c, h)

        ident = const.tile([P, P], F32)
        make_identity(nc, ident[:])
        zeros = const.tile([P, CH], BF16)
        nc.vector.memset(zeros[:].bitcast(I32), 0)
        table = const.tile([P, 1], F32)
        nc.vector.memset(table[:], 0.0)
        nc.scalar.activation(out=table[:], in_=table[:], func=ACT.Exp)
        ident16 = const.tile([P, P], BF16)
        nc.vector.tensor_copy(out=ident16[:], in_=ident[:])

        x_codes = const.tile([P, NG, TOKENS], U32, align_bytes=64)
        x_scales = const.tile([P, NG, TOKENS], U8, align_bytes=64)
        a_codes = const.tile([P, NT, NG * P], U32, align_bytes=64)
        a_scales = const.tile([P, NT, NG * P], U8, align_bytes=64)
        b_codes = const.tile([P, O], U32, align_bytes=64)
        b_scales = const.tile([P, O], U8, align_bytes=64)
        h_codes = const.tile([P, TOKENS], U32, align_bytes=64)
        h_scales = const.tile([P, TOKENS], U8, align_bytes=64)
        routed = const.tile([P, NT, TOKENS], BF16)
        routed_mix = const.tile([P, 4 * TOKENS], BF16, align_bytes=64)
        route_t = const.tile([P, TOKENS], F32)
        route = const.tile([P, NT, E, 4], F32)
        weights = const.tile([P, NT, E], F32)
        chunk0 = const.tile([P, NT, CH], F32)
        bias = const.tile([P, O], BF16)

        def copy(engine, dst, src):
            if engine == "v":
                nc.vector.tensor_copy(out=dst, in_=src)
            else:
                nc.scalar.copy(out=dst, in_=src)

        def new_acc(key):
            bank = acc_pool.tile([P, CH], F32, tag="acc")
            acc[key] = bank
            return bank

        def new_grouped(key):
            tile = grouped_pool.tile([P, 8192], BF16, tag="grouped", align_bytes=64)
            grouped[key] = tile

        def softmax():
            top = const.tile([P, NT], F32)
            nc.vector.tensor_reduce(out=top[:], in_=gates[:], axis=AX.X, op=ALU.max)
            shifted = const.tile([P, NT, E], F32)
            nc.vector.tensor_tensor(out=shifted[:], in0=gates[:], in1=top[:].unsqueeze(2).to_broadcast([P, NT, E]), op=ALU.subtract)
            nc.scalar.activation(out=weights[:], in_=shifted[:], func=ACT.Exp)
            total = const.tile([P, NT], F32)
            nc.vector.tensor_reduce(out=total[:], in_=weights[:], axis=AX.X, op=ALU.add)
            inverse = const.tile([P, NT], F32)
            nc.vector.reciprocal(out=inverse[:], in_=total[:])
            factor = const.tile([P, NT], F32)
            nc.vector.tensor_scalar_mul(out=factor[:], in0=inverse[:], scalar1=SCALING)
            nc.vector.tensor_tensor(
                out=route[:],
                in0=weights[:].unsqueeze(3).to_broadcast([P, NT, E, 4]),
                in1=factor[:].unsqueeze(2).unsqueeze(3).to_broadcast([P, NT, E, 4]),
                op=ALU.mult,
            )

        def idle_product(bank):
            nc.tensor.matmul(out=bank[:], lhsT=zeros[:, 0:P], rhs=zeros[:], start=True, stop=True)

        def bias_product(c):
            bank = new_acc(("bias", c))
            nc.tensor.matmul(out=bank[:], lhsT=ident16[:, c:c + 1].to_broadcast([P, P]), rhs=bias_rows[:], start=True, stop=True)

        def bias_out(c, engine):
            copy(engine, bias[:, c * CH:(c + 1) * CH], acc["bias", c][:])

        def xa_words(kind, t):
            first = 0 if kind == "x" else D // 2
            return raw["xa", t][:].bitcast(F32)[:, first:first + D // 2]

        def split_a(t):
            tile = split_pool.tile([P, D], F32, tag="split")
            split["a", t] = tile
            src = xa_words("a", t).rearrange("p (g n u) -> p g n u", g=NG, u=2)
            copy("v", tile[:, 0:D // 2].rearrange("p (g u n) -> p g n u", g=NG, u=2), src)

        def turn_xa(kind, t, engines):
            order = "p (g t n u) -> p t g n u" if kind == "x" else "p (t g n u) -> p t g n u"
            dst = grouped[kind][:].bitcast(F32).rearrange(order, g=NG, t=NT, u=2)[:, t]
            for b in range(2):
                bank = turn_pool.tile([P, CH], F32, tag="turn")
                for i in range(4):
                    g, u = 2 * b + i // 2, i % 2
                    if (kind, t) in split:
                        words = split[kind, t][:, (2 * g + u) * P:(2 * g + u + 1) * P]
                    else:
                        words = xa_words(kind, t)[:, 256 * g + u:256 * (g + 1):2]
                    nc.tensor.transpose(bank[:, i * P:(i + 1) * P], words, ident[:])
                copy(engines[b], dst[:, 2 * b:2 * b + 2], bank[:].rearrange("p (g u n) -> p g n u", g=2, u=2))

        def quantize_x(pair):
            tokens = slice(pair * 2 * P, (pair + 1) * 2 * P)
            for g in range(NG):
                first = g * 2048 + pair * 1024
                nc.vector.quantize_mx(
                    out=x_codes[:, g, tokens].bitcast(FP8X4),
                    scales=x_scales[:, g, tokens],
                    in_=grouped["x"][:, first:first + 1024],
                )

        def quantize_a(t):
            nc.vector.quantize_mx(
                out=a_codes[:, t, :].bitcast(FP8X4),
                scales=a_scales[:, t, :],
                in_=grouped["a"][:, t * 2048:(t + 1) * 2048],
            )

        def split_w(c, h, engines):
            tile = split_pool.tile([P, D], F32, tag="split")
            split["w", c, h] = tile
            src = raw["w", c, h][:].bitcast(F32).rearrange("p (j g n u) -> p g j n u", j=2, g=NG, u=2)
            dst = tile[:].rearrange("p (g j u n) -> p g j n u", g=NG, j=2, u=2)
            for k in range(2):
                copy(engines[k], dst[:, 2 * k:2 * k + 2], src[:, 2 * k:2 * k + 2])

        def turn_w(c, h):
            if h == 0:
                new_grouped(("w", c))
            dst = grouped["w", c][:].bitcast(F32).rearrange("p (g n j u) -> p g n j u", g=NG, j=4, u=2)
            for g in range(NG):
                bank = turn_pool.tile([P, CH], F32, tag="turn")
                for i in range(4):
                    words = split["w", c, h][:, (4 * g + i) * P:(4 * g + i + 1) * P]
                    nc.tensor.transpose(bank[:, i * P:(i + 1) * P], words, ident[:])
                copy("s", dst[:, g, :, 2 * h:2 * h + 2, :], bank[:].rearrange("p (j u n) -> p n j u", j=2, u=2))

        def quantize_w(c, passes):
            if 0 in passes:
                w_codes = code_pool.tile([P, NG * CH], U32, tag="codes", align_bytes=64)
                w_scales = code_pool.tile([P, NG * CH], U8, tag="scales", align_bytes=64)
                codes[c] = (w_codes, w_scales)
            w_codes, w_scales = codes[c]
            for g in passes:
                nc.vector.quantize_mx(
                    out=w_codes[:, g * CH:(g + 1) * CH].bitcast(FP8X4),
                    scales=w_scales[:, g * CH:(g + 1) * CH],
                    in_=grouped["w", c][:, g * 2048:(g + 1) * 2048],
                )

        def split_b(h, engines):
            src = raw["b", h][:].bitcast(F32).rearrange("p (e s v u) -> p s e v u", e=16, s=16, v=4)
            for k in range(2):
                if h == 0:
                    tile = split_pool.tile([P, D], F32, tag="split")
                    split["b", k] = tile
                dst = split["b", k][:].rearrange("p (s u e v) -> p s e v u", s=8, u=2, v=4)
                copy(engines[k], dst[:, :, 16 * h:16 * h + 16], src[:, 8 * k:8 * k + 8])

        def turn_b(k):
            if k == 0:
                new_grouped("b")
            dst = grouped["b"][:].bitcast(F32).rearrange("p (n s u) -> p n s u", s=16, u=2)
            for b in range(4):
                bank = turn_pool.tile([P, CH], F32, tag="turn")
                for i in range(4):
                    words = split["b", k][:, (4 * b + i) * P:(4 * b + i + 1) * P]
                    nc.tensor.transpose(bank[:, i * P:(i + 1) * P], words, ident[:])
                s = 8 * k + 2 * b
                copy("sv"[b % 2], dst[:, :, s:s + 2, :], bank[:].rearrange("p (s u n) -> p n s u", s=2, u=2))

        def quantize_b(c):
            nc.vector.quantize_mx(
                out=b_codes[:, c * CH:(c + 1) * CH].bitcast(FP8X4),
                scales=b_scales[:, c * CH:(c + 1) * CH],
                in_=grouped["b"][:, c * 2048:(c + 1) * 2048],
            )

        def h_product(t):
            bank = new_acc(("h", t))
            for g in range(NG):
                nc.tensor.matmul_mx(
                    out=bank[:],
                    lhsT=a_codes[:, t, g * P:(g + 1) * P].bitcast(FP8X4),
                    lhsT_scale=a_scales[:, t, g * P:(g + 1) * P],
                    rhs=x_codes[:, g, :].bitcast(FP8X4),
                    rhs_scale=x_scales[:, g, :],
                    start=(g == 0),
                    stop=(g == NG - 1),
                )

        def turn_route():
            bank = turn_pool.tile([P, CH], F32, tag="turn")
            idle_product(bank)
            rows = route[:].rearrange("p t e i -> p t (e i)")
            for t in range(NT):
                nc.tensor.transpose(bank[:, t * P:(t + 1) * P], rows[:, t, :], ident[:])
            nc.scalar.copy(out=route_t[:], in_=bank[:])

        def h_route(t):
            nc.vector.tensor_tensor(out=routed[:, t, :], in0=acc["h", t][:], in1=route_t[:], op=ALU.mult)

        def h_mix(half, engine):
            tokens = slice(half * 256, (half + 1) * 256)
            copy(
                engine,
                routed_mix[:, half * 1024:(half + 1) * 1024].rearrange("p (n t) -> p n t", t=4),
                routed[:, :, tokens].rearrange("p t n -> p n t"),
            )

        def h_quantize():
            nc.vector.quantize_mx(out=h_codes[:].bitcast(FP8X4), scales=h_scales[:], in_=routed_mix[:])

        def base_passes(bank, c, t, first, width, last):
            w_codes, w_scales = codes[c]
            for g in range(NG):
                cols = slice(g * CH + first, g * CH + first + width)
                nc.tensor.matmul_mx(
                    out=bank[:, 0:width],
                    lhsT=x_codes[:, g, t * P:(t + 1) * P].bitcast(FP8X4),
                    lhsT_scale=x_scales[:, g, t * P:(t + 1) * P],
                    rhs=w_codes[:, cols].bitcast(FP8X4),
                    rhs_scale=w_scales[:, cols],
                    start=(g == 0),
                    stop=(last and g == NG - 1),
                )

        def adapter_pass(bank, c, t, first, width, alone):
            cols = slice(c * CH + first, c * CH + first + width)
            nc.tensor.matmul_mx(
                out=bank[:, 0:width],
                lhsT=h_codes[:, t * P:(t + 1) * P].bitcast(FP8X4),
                lhsT_scale=h_scales[:, t * P:(t + 1) * P],
                rhs=b_codes[:, cols].bitcast(FP8X4),
                rhs_scale=b_scales[:, cols],
                start=alone,
                stop=True,
            )

        def base(c, t, last=False):
            base_passes(new_acc((c, t)), c, t, 0, CH, last)

        def adapter(c, t):
            adapter_pass(acc[c, t], c, t, 0, CH, alone=False)

        def both(c, t):
            base(c, t)
            adapter(c, t)

        def store(c, t, first, width, tile):
            cols = slice(c * CH + first, c * CH + first + width)
            nc.sync.dma_start(out=out_rows[t * P:(t + 1) * P, cols], in_=tile[:])

        def finish(c, t):
            tile = out_pool.tile([P, CH], F32, tag="out")
            nc.vector.tensor_tensor(out=tile[:], in0=acc[c, t][:], in1=bias[:, c * CH:(c + 1) * CH], op=ALU.add)
            store(c, t, 0, CH, tile)

        def finish_base0(t):
            nc.vector.tensor_tensor(out=chunk0[:, t, :], in0=acc[0, t][:], in1=bias[:, 0:CH], op=ALU.add)

        def adapter0(t):
            adapter_pass(new_acc((0, t)), 0, t, 0, CH, alone=True)

        def finish0(t):
            tile = out_pool.tile([P, CH], F32, tag="out")
            nc.vector.tensor_tensor(out=tile[:], in0=acc[0, t][:], in1=chunk0[:, t, :], op=ALU.add)
            store(0, t, 0, CH, tile)

        HALF = CH // 2

        def both_half(c, t, k):
            bank = new_acc((c, t, k))
            base_passes(bank, c, t, k * HALF, HALF, last=False)
            adapter_pass(bank, c, t, k * HALF, HALF, alone=False)

        def finish_half(c, t, k):
            tile = out_pool.tile([P, HALF], F32, tag="out")
            cols = slice(c * CH + k * HALF, c * CH + (k + 1) * HALF)
            nc.vector.tensor_tensor(out=tile[:], in0=acc[c, t, k][:, 0:HALF], in1=bias[:, cols], op=ALU.add)
            store(c, t, k * HALF, HALF, tile)

        idle_bank = turn_pool.tile([P, CH], F32, tag="turn")
        for i in range(3):
            idle_product(idle_bank)
        softmax()
        new_grouped("x")
        new_grouped("a")
        turn_xa("x", 0, "ss")
        bias_product(0)
        bias_product(1)
        bias_out(0, "v")
        bias_out(1, "v")
        turn_xa("x", 1, "ss")
        quantize_x(0)
        turn_xa("x", 2, "sv")
        turn_xa("x", 3, "sv")
        turn_xa("a", 0, "ss")
        bias_product(2)
        turn_xa("a", 1, "ss")
        bias_product(3)
        quantize_x(1)
        quantize_a(0)
        split_a(3)
        turn_xa("a", 2, "ss")
        quantize_a(1)
        turn_route()
        bias_out(2, "v")
        bias_out(3, "s")
        load_b(0)
        load_b(1)
        load_w(2, 0)
        load_w(2, 1)
        h_product(0)
        turn_xa("a", 3, "ss")
        split_w(0, 0, "vv")
        h_route(0)
        quantize_a(2)
        h_product(1)
        turn_w(0, 0)
        split_w(0, 1, "vv")
        quantize_a(3)
        h_route(1)
        h_product(2)
        turn_w(0, 1)
        split_w(1, 0, "vv")
        h_product(3)
        h_route(2)
        quantize_w(0, (0, 1, 2, 3))
        h_route(3)

        turn_w(1, 0)
        split_w(1, 1, "vv")
        base(0, 0, last=True)
        base(0, 1, last=True)
        finish_base0(0)
        finish_base0(1)
        load_w(3, 0)
        split_b(0, "vs")
        turn_w(1, 1)
        base(0, 2, last=True)
        base(0, 3, last=True)
        quantize_w(1, (0, 1, 2, 3))
        finish_base0(2)
        split_b(1, "vs")
        finish_base0(3)
        load_w(3, 1)
        split_w(2, 0, "vs")
        base(1, 0)
        base(1, 1)
        turn_b(0)
        h_mix(0, "s")
        h_mix(1, "v")
        base(1, 2)
        split_w(2, 1, "vs")
        h_quantize()
        turn_b(1)
        quantize_b(1)
        base(1, 3)
        turn_w(2, 0)
        split_w(3, 0, "vv")
        quantize_b(0)
        for t in range(NT):
            adapter(1, t)
        for t in range(NT):
            finish(1, t)

        turn_w(2, 1)
        quantize_w(2, (0, 1, 2, 3))
        quantize_b(2)
        adapter0(0)
        adapter0(1)
        turn_w(3, 0)
        split_w(3, 1, "vs")
        both(2, 0)
        both(2, 1)
        finish0(0)
        finish(2, 0)
        finish0(1)
        finish(2, 1)
        turn_w(3, 1)
        quantize_b(3)
        both(2, 2)
        both(2, 3)
        quantize_w(3, (0, 1))
        finish(2, 2)
        quantize_w(3, (2, 3))
        finish(2, 3)
        adapter0(2)
        adapter0(3)
        finish0(2)
        finish0(3)
        both(3, 0)
        both(3, 1)
        finish(3, 0)
        finish(3, 1)
        both(3, 2)
        both_half(3, 3, 0)
        both_half(3, 3, 1)
        finish(3, 2)
        finish_half(3, 3, 0)
        finish_half(3, 3, 1)
